import numpy as np
import ml_dtypes


def mxq(x, axis, fmt="e4m3"):
    dtype, down = {"e4m3": (ml_dtypes.float8_e4m3fn, 7), "e5m2": (ml_dtypes.float8_e5m2, 14)}[fmt]
    v = np.moveaxis(np.asarray(x, np.float32).astype(ml_dtypes.bfloat16).astype(np.float64), axis, -1)
    blocks = v.reshape(v.shape[:-1] + (-1, 32))
    amax = np.abs(blocks).max(-1, keepdims=True)
    byte = np.maximum(np.where(amax > 0, np.frexp(amax)[1] - 1 + 127, 0) - down, 1)
    scale = np.exp2(byte - 127.0)
    codes = (blocks / scale).astype(np.float32).astype(dtype).astype(np.float64)
    return np.moveaxis((codes * scale).reshape(v.shape), -1, axis)


WIDE = False


def mx_kscale(k):
    if not WIDE:
        return np.ones(k)
    levels = np.array([10, -10, 5, -5, 0])
    a = np.random.permutation(np.resize(levels, k // 512 * 4)).reshape(k // 512, 4)
    idx = np.arange(k)
    return np.exp2(a[idx // 512, idx % 128 // 32])


BF16 = ml_dtypes.bfloat16


def bf(x):
    return np.asarray(x, np.float32).astype(BF16)


def f64(x):
    return np.asarray(x).astype(np.float64)


B, N, R, F = 2, 8, 512, 1024
GAMMA = 10.0
STEP = 0.1
LOG2 = np.log(2.0)


def ssp(v):
    return np.maximum(v, 0.0) + np.log(1.0 + np.exp(-np.abs(v))) - LOG2


def setup_inputs():
    t = mx_kscale(F)
    t = t / t.min()
    return {"x": bf(np.random.standard_normal((B, N, F))),
            "distances": bf(np.random.uniform(0.0, STEP * R, (B, N, N))),
            "W1": bf(np.random.standard_normal((R, F)) * 0.5 * t[None, :]),
            "b1": bf(np.random.standard_normal(F) * 0.2 * t),
            "W2": bf(np.random.standard_normal((F, F)) * 2.0 / np.sqrt(F) / t[:, None]),
            "b2": bf(np.random.standard_normal(F) * 0.2)}


def reference(x, distances, W1, b1, W2, b2):
    centers = STEP * np.arange(R)
    e_k = np.exp(-GAMMA * (f64(distances)[..., None] - centers) ** 2)
    h = ssp((mxq(e_k, 3, "e4m3") @ mxq(f64(W1), 0, "e4m3")) + f64(b1))
    w_l = ssp((mxq(h, 3, "e4m3") @ mxq(f64(W2), 0, "e4m3")) + f64(b2))
    return np.sum(f64(x)[:, :, None, :] * w_l, axis=2)

@@ -1,0 +1,228 @@
+import concourse.mybir as mybir
+from concourse.masks import make_identity
+
+F32 = mybir.dt.float32
+BF16 = mybir.dt.bfloat16
+I32 = mybir.dt.int32
+U32 = mybir.dt.uint32
+U8 = mybir.dt.uint8
+FP8X4 = mybir.dt.float8_e4m3fn_x4
+ACT = mybir.ActivationFunctionType
+ALU = mybir.AluOpType
+AXIS = mybir.AxisListType
+
+P = 128
+PACK = 4
+K_PASS = P * PACK
+
+ATOMS = 8
+ROWS = 16
+PAIRS = ROWS * ATOMS
+BASIS = 512
+FEATURES = 1024
+CHUNKS = FEATURES // P
+SLABS = 3
+PIECE = 512
+RUN = 4
+GROUP = PIECE // P
+GROUPS = CHUNKS // GROUP
+assert GROUP * P == K_PASS
+
+FLOPS = 2 * PAIRS * BASIS * FEATURES + 2 * PAIRS * FEATURES * FEATURES
+
+
+def tile_cfconv_pa_s_kernel(tc, x, distances, W1, b1, W2, b2, out):
+    nc = tc.nc
+    with tc.tile_pool(name="keep", bufs=1) as keep, tc.psum_pool(name="banks", bufs=8) as banks, tc.manual_schedule():
+        d_column = keep.tile([P, 1], BF16)
+        nc.scalar.dma_start(out=d_column[:], in_=distances.rearrange("b i (j o) -> (b i j) o", o=1))
+
+        slab_rows = [
+            W1.rearrange("(p t) f -> p t f", t=PACK),
+            W2[0:K_PASS, :].rearrange("(t p) f -> p t f", p=P),
+            W2[K_PASS : 2 * K_PASS, :].rearrange("(t p) f -> p t f", p=P),
+        ]
+        raw = keep.tile([P, SLABS, PACK, FEATURES], BF16)
+        pieces = [(s, slice(c, c + PIECE)) for s in range(SLABS) for c in range(0, FEATURES, PIECE)]
+        w1_pieces = [piece for piece in pieces if piece[0] == 0]
+        w2_pieces = [piece for piece in pieces if piece[0] > 0]
+
+        def load(piece):
+            s, cols = piece
+            nc.sync.dma_start(out=raw[:, s, :, cols], in_=slab_rows[s][:, :, cols])
+
+        for piece in w1_pieces:
+            load(piece)
+        bias_rows = keep.tile([P, P], BF16)
+        nc.vector.memset(bias_rows[:], 0.0)
+        nc.sync.dma_start(out=bias_rows[0:CHUNKS, :], in_=b1.rearrange("(m p) -> m p", p=P))
+        nc.sync.dma_start(out=bias_rows[CHUNKS : 2 * CHUNKS, :], in_=b2.rearrange("(m p) -> m p", p=P))
+        for piece in w2_pieces:
+            load(piece)
+        x_rows = keep.tile([P, P], BF16)
+        nc.sync.dma_start(out=x_rows[:], in_=x.rearrange("b i (c p) -> (b i c) p", p=P))
+
+        minus_k_int = keep.tile([P, PACK], I32)
+        nc.gpsimd.iota(minus_k_int[:], pattern=[[-1, PACK]], base=0, channel_multiplier=-PACK)
+        minus_k = keep.tile([P, PACK], F32)
+        nc.vector.tensor_copy(out=minus_k[:], in_=minus_k_int[:])
+        ident_bf = keep.tile([P, P], BF16)
+        make_identity(nc, ident_bf[:])
+        ident_f32 = keep.tile([P, P], F32)
+        make_identity(nc, ident_f32[:])
+
+        d_all = banks.tile([P, PAIRS], F32, tag="bank")
+        nc.tensor.matmul(out=d_all[:], lhsT=d_column[:, 0:1].to_broadcast([P, P]), rhs=ident_bf[:], start=True, stop=True)
+        square = keep.tile([P, PACK, PAIRS], F32)
+        for t in range(PACK):
+            nc.scalar.activation(
+                out=square[:, t, :], in_=d_all[:], func=ACT.Square, scale=10.0, bias=minus_k[:, t : t + 1]
+            )
+        e_grouped = keep.tile([P, PAIRS, PACK], BF16, align_bytes=64)
+        nc.scalar.activation(out=e_grouped[:], in_=square[:].rearrange("p t r -> p r t"), func=ACT.Exp, scale=-0.1)
+        e_codes = keep.tile([P, PAIRS], U32, align_bytes=64)
+        e_scales = keep.tile([P, PAIRS], U8, align_bytes=64)
+
+        bias_turned = banks.tile([P, P], BF16, tag="bank")
+        nc.tensor.transpose(out=bias_turned[:], in_=bias_rows[:], identity=ident_bf[:])
+        bias = keep.tile([P, 2 * CHUNKS], F32)
+        nc.scalar.copy(out=bias[:], in_=bias_turned[:, 0 : 2 * CHUNKS])
+
+        grouped = keep.tile([P, SLABS, FEATURES, PACK], BF16, align_bytes=64)
+        w_codes = keep.tile([P, SLABS, FEATURES], U32, align_bytes=64)
+        w_scales = keep.tile([P, SLABS, FEATURES], U8, align_bytes=64)
+
+        def regroup(piece):
+            s, cols = piece
+            nc.vector.tensor_copy(
+                out=grouped[:, s, cols, :].rearrange("p (c i) t -> p c t i", i=RUN),
+                in_=raw[:, s, :, cols].rearrange("p t (c i) -> p c t i", i=RUN),
+            )
+
+        def quantise(piece):
+            s, cols = piece
+            nc.vector.quantize_mx(
+                out=w_codes[:, s, cols].bitcast(FP8X4),
+                scales=w_scales[:, s, cols],
+                in_=grouped[:, s, cols, :].rearrange("p c t -> p (c t)"),
+            )
+
+        pre1 = keep.tile([P, CHUNKS, PAIRS], F32)
+        size1 = keep.tile([P, CHUNKS, PAIRS], F32)
+        decay1 = keep.tile([P, CHUNKS, PAIRS], F32)
+        log1 = keep.tile([P, CHUNKS, PAIRS], F32)
+
+        def first_layer(g):
+            chunks = slice(g * GROUP, (g + 1) * GROUP)
+            for m in range(g * GROUP, (g + 1) * GROUP):
+                m_cols = slice(m * P, (m + 1) * P)
+                v1 = banks.tile([P, PAIRS], F32, tag="bank")
+                nc.tensor.matmul_mx(
+                    out=v1[:],
+                    lhsT=w_codes[:, 0, m_cols].bitcast(FP8X4),
+                    lhsT_scale=w_scales[:, 0, m_cols],
+                    rhs=e_codes[:].bitcast(FP8X4),
+                    rhs_scale=e_scales[:],
+                    start=True,
+                    stop=True,
+                )
+                nc.scalar.activation(out=pre1[:, m, :], in_=v1[:], func=ACT.Identity, bias=bias[:, m : m + 1])
+            nc.scalar.activation(out=size1[:, chunks, :], in_=pre1[:, chunks, :], func=ACT.Abs)
+            nc.scalar.activation(out=decay1[:, chunks, :], in_=size1[:, chunks, :], func=ACT.Exp, scale=-1.0)
+
+        regroup(w1_pieces[0])
+        nc.vector.quantize_mx(
+            out=e_codes[:].bitcast(FP8X4), scales=e_scales[:], in_=e_grouped[:].rearrange("p r t -> p (r t)")
+        )
+        quantise(w1_pieces[0])
+        first_layer(0)
+        regroup(w1_pieces[1])
+        regroup(w2_pieces[0])
+        quantise(w1_pieces[1])
+        first_layer(1)
+        for g in range(GROUPS):
+            chunks = slice(g * GROUP, (g + 1) * GROUP)
+            nc.scalar.activation(out=log1[:, chunks, :], in_=decay1[:, chunks, :], func=ACT.Ln, scale=0.5, bias=0.5)
+        table_warmer = keep.tile([P, 1], F32)
+        nc.scalar.activation(out=table_warmer[:], in_=minus_k[:, 0:1], func=ACT.Sigmoid)
+
+        for i in range(1, len(w2_pieces)):
+            regroup(w2_pieces[i])
+            quantise(w2_pieces[i - 1])
+
+        h_grouped = keep.tile([P, GROUPS, PAIRS, PACK], BF16, align_bytes=64)
+        h_codes = keep.tile([P, GROUPS, PAIRS], U32, align_bytes=64)
+        h_scales = keep.tile([P, GROUPS, PAIRS], U8, align_bytes=64)
+        for g in range(GROUPS):
+            chunks = slice(g * GROUP, (g + 1) * GROUP)
+            nc.vector.scalar_tensor_tensor(
+                out=h_grouped[:, g, :, :],
+                in0=pre1[:, chunks, :].rearrange("p t r -> p r t"),
+                scalar=0.0,
+                in1=log1[:, chunks, :].rearrange("p t r -> p r t"),
+                op0=ALU.max,
+                op1=ALU.add,
+            )
+        for g in range(GROUPS):
+            nc.vector.quantize_mx(
+                out=h_codes[:, g, :].bitcast(FP8X4),
+                scales=h_scales[:, g, :],
+                in_=h_grouped[:, g, :, :].rearrange("p r t -> p (r t)"),
+            )
+        quantise(w2_pieces[-1])
+
+        size2 = keep.tile([P, CHUNKS, PAIRS], F32)
+        twice2 = keep.tile([P, CHUNKS, PAIRS], F32)
+        gate2 = keep.tile([P, CHUNKS, PAIRS], F32)
+        product = keep.tile([P, CHUNKS, ROWS], F32)
+        twice_sum = keep.tile([P, CHUNKS, ROWS], F32)
+        for group in range(GROUPS):
+            chunks = slice(group * GROUP, (group + 1) * GROUP)
+            for c in range(group * GROUP, (group + 1) * GROUP):
+                c_cols = slice(c * P, (c + 1) * P)
+                b2_c = bias[:, CHUNKS + c : CHUNKS + c + 1]
+                v2 = banks.tile([P, PAIRS], F32, tag="bank")
+                for g in range(GROUPS):
+                    nc.tensor.matmul_mx(
+                        out=v2[:],
+                        lhsT=w_codes[:, 1 + g, c_cols].bitcast(FP8X4),
+                        lhsT_scale=w_scales[:, 1 + g, c_cols],
+                        rhs=h_codes[:, g, :].bitcast(FP8X4),
+                        rhs_scale=h_scales[:, g, :],
+                        start=(g == 0),
+                        stop=(g == GROUPS - 1),
+                    )
+                nc.scalar.activation(out=size2[:, c, :], in_=v2[:], func=ACT.Abs, bias=b2_c)
+                nc.vector.scalar_tensor_tensor(
+                    out=twice2[:, c, :], in0=v2[:], scalar=b2_c, in1=size2[:, c, :], op0=ALU.add, op1=ALU.add
+                )
+            nc.scalar.activation(out=gate2[:, chunks, :], in_=size2[:, chunks, :], func=ACT.Sigmoid)
+            nc.vector.tensor_reduce(
+                out=twice_sum[:, chunks, :].rearrange("p c r -> p (c r)"),
+                in_=twice2[:, chunks, :].rearrange("p c (r j) -> p (c r) j", j=ATOMS),
+                axis=AXIS.X,
+                op=ALU.add,
+            )
+            nc.vector.tensor_reduce(
+                out=product[:, chunks, :].rearrange("p c r -> p (c r)"),
+                in_=gate2[:, chunks, :].rearrange("p c (r j) -> p (c r) j", j=ATOMS),
+                axis=AXIS.X,
+                op=ALU.mult,
+            )
+        log_product = keep.tile([P, CHUNKS, ROWS], F32)
+        nc.scalar.activation(out=log_product[:], in_=product[:], func=ACT.Ln, scale=float(2**ATOMS))
+        summed = keep.tile([P, ROWS, CHUNKS], F32)
+        nc.vector.scalar_tensor_tensor(
+            out=summed[:],
+            in0=twice_sum[:].rearrange("p c r -> p r c"),
+            scalar=0.5,
+            in1=log_product[:].rearrange("p c r -> p r c"),
+            op0=ALU.mult,
+            op1=ALU.subtract,
+        )
+
+        turned = banks.tile([P, P], F32, tag="bank")
+        nc.tensor.transpose(out=turned[:], in_=summed[:].rearrange("p r c -> p (r c)"), identity=ident_f32[:])
+        result = keep.tile([P, P], F32)
+        nc.vector.tensor_tensor(out=result[:], in0=turned[:], in1=x_rows[:], op=ALU.mult)
+        nc.sync.dma_start(out=out.rearrange("b i (c p) -> (b i c) p", p=P), in_=result[:])

@@ -20,15 +20,18 @@ ROWS = 16
 PAIRS = ROWS * ATOMS
 BASIS = 512
 FEATURES = 1024
+PASSES = FEATURES // K_PASS
 CHUNKS = FEATURES // P
-SLABS = 3
-PIECE = 512
+SLABS = 1 + PASSES
+BIG = 512
+SMALL = 256
 RUN = 4
-GROUP = PIECE // P
-GROUPS = CHUNKS // GROUP
-assert GROUP * P == K_PASS
 
 FLOPS = 2 * PAIRS * BASIS * FEATURES + 2 * PAIRS * FEATURES * FEATURES
+
+
+def chunks_of(first_column, width):
+    return range(first_column // P, (first_column + width) // P)
 
 
 def tile_cfconv_pa_s_kernel(tc, x, distances, W1, b1, W2, b2, out):
@@ -43,22 +46,23 @@ def tile_cfconv_pa_s_kernel(tc, x, distances, W1, b1, W2, b2, out):
             W2[K_PASS : 2 * K_PASS, :].rearrange("(t p) f -> p t f", p=P),
         ]
         raw = keep.tile([P, SLABS, PACK, FEATURES], BF16)
-        pieces = [(s, slice(c, c + PIECE)) for s in range(SLABS) for c in range(0, FEATURES, PIECE)]
-        w1_pieces = [piece for piece in pieces if piece[0] == 0]
-        w2_pieces = [piece for piece in pieces if piece[0] > 0]
 
-        def load(piece):
-            s, cols = piece
-            nc.sync.dma_start(out=raw[:, s, :, cols], in_=slab_rows[s][:, :, cols])
+        def load(slab, first, width):
+            cols = slice(first, first + width)
+            nc.sync.dma_start(out=raw[:, slab, :, cols], in_=slab_rows[slab][:, :, cols])
 
-        for piece in w1_pieces:
-            load(piece)
+        w1_units = [(0, first, SMALL) for first in range(0, FEATURES, SMALL)]
+        load(*w1_units[0])
+        load(*w1_units[1])
         bias_rows = keep.tile([P, P], BF16)
         nc.vector.memset(bias_rows[:], 0.0)
         nc.sync.dma_start(out=bias_rows[0:CHUNKS, :], in_=b1.rearrange("(m p) -> m p", p=P))
         nc.sync.dma_start(out=bias_rows[CHUNKS : 2 * CHUNKS, :], in_=b2.rearrange("(m p) -> m p", p=P))
-        for piece in w2_pieces:
-            load(piece)
+        load(*w1_units[2])
+        load(*w1_units[3])
+        for slab in range(1, SLABS):
+            for first in range(0, FEATURES, BIG):
+                load(slab, first, BIG)
         x_rows = keep.tile([P, P], BF16)
         nc.sync.dma_start(out=x_rows[:], in_=x.rearrange("b i (c p) -> (b i c) p", p=P))
 
@@ -92,19 +96,19 @@ def tile_cfconv_pa_s_kernel(tc, x, distances, W1, b1, W2, b2, out):
         w_codes = keep.tile([P, SLABS, FEATURES], U32, align_bytes=64)
         w_scales = keep.tile([P, SLABS, FEATURES], U8, align_bytes=64)
 
-        def regroup(piece):
-            s, cols = piece
+        def regroup(slab, first, width):
+            cols = slice(first, first + width)
             nc.vector.tensor_copy(
-                out=grouped[:, s, cols, :].rearrange("p (c i) t -> p c t i", i=RUN),
-                in_=raw[:, s, :, cols].rearrange("p t (c i) -> p c t i", i=RUN),
+                out=grouped[:, slab, cols, :].rearrange("p (c i) t -> p c t i", i=RUN),
+                in_=raw[:, slab, :, cols].rearrange("p t (c i) -> p c t i", i=RUN),
             )
 
-        def quantise(piece):
-            s, cols = piece
+        def quantise(slab, first, width):
+            cols = slice(first, first + width)
             nc.vector.quantize_mx(
-                out=w_codes[:, s, cols].bitcast(FP8X4),
-                scales=w_scales[:, s, cols],
-                in_=grouped[:, s, cols, :].rearrange("p c t -> p (c t)"),
+                out=w_codes[:, slab, cols].bitcast(FP8X4),
+                scales=w_scales[:, slab, cols],
+                in_=grouped[:, slab, cols, :].rearrange("p c t -> p (c t)"),
             )
 
         pre1 = keep.tile([P, CHUNKS, PAIRS], F32)
@@ -112,49 +116,63 @@ def tile_cfconv_pa_s_kernel(tc, x, distances, W1, b1, W2, b2, out):
         decay1 = keep.tile([P, CHUNKS, PAIRS], F32)
         log1 = keep.tile([P, CHUNKS, PAIRS], F32)
 
-        def first_layer(g):
-            chunks = slice(g * GROUP, (g + 1) * GROUP)
-            for m in range(g * GROUP, (g + 1) * GROUP):
+        def first_matmul(slab, first, width):
+            for m in chunks_of(first, width):
                 m_cols = slice(m * P, (m + 1) * P)
                 v1 = banks.tile([P, PAIRS], F32, tag="bank")
                 nc.tensor.matmul_mx(
                     out=v1[:],
-                    lhsT=w_codes[:, 0, m_cols].bitcast(FP8X4),
-                    lhsT_scale=w_scales[:, 0, m_cols],
+                    lhsT=w_codes[:, slab, m_cols].bitcast(FP8X4),
+                    lhsT_scale=w_scales[:, slab, m_cols],
                     rhs=e_codes[:].bitcast(FP8X4),
                     rhs_scale=e_scales[:],
                     start=True,
                     stop=True,
                 )
                 nc.scalar.activation(out=pre1[:, m, :], in_=v1[:], func=ACT.Identity, bias=bias[:, m : m + 1])
+
+        def pass_chunks(g):
+            return slice(g * PACK, (g + 1) * PACK)
+
+        def first_decay(g):
+            chunks = pass_chunks(g)
             nc.scalar.activation(out=size1[:, chunks, :], in_=pre1[:, chunks, :], func=ACT.Abs)
             nc.scalar.activation(out=decay1[:, chunks, :], in_=size1[:, chunks, :], func=ACT.Exp, scale=-1.0)
 
-        regroup(w1_pieces[0])
+        regroup(*w1_units[0])
+        regroup(*w1_units[1])
+        quantise(*w1_units[0])
+        regroup(*w1_units[2])
         nc.vector.quantize_mx(
             out=e_codes[:].bitcast(FP8X4), scales=e_scales[:], in_=e_grouped[:].rearrange("p r t -> p (r t)")
         )
-        quantise(w1_pieces[0])
-        first_layer(0)
-        regroup(w1_pieces[1])
-        regroup(w2_pieces[0])
-        quantise(w1_pieces[1])
-        first_layer(1)
-        for g in range(GROUPS):
-            chunks = slice(g * GROUP, (g + 1) * GROUP)
+        first_matmul(*w1_units[0])
+        quantise(*w1_units[1])
+        first_matmul(*w1_units[1])
+        first_decay(0)
+        regroup(*w1_units[3])
+        quantise(*w1_units[2])
+        first_matmul(*w1_units[2])
+        quantise(*w1_units[3])
+        first_matmul(*w1_units[3])
+        first_decay(1)
+        for g in range(PASSES):
+            chunks = pass_chunks(g)
             nc.scalar.activation(out=log1[:, chunks, :], in_=decay1[:, chunks, :], func=ACT.Ln, scale=0.5, bias=0.5)
-        table_warmer = keep.tile([P, 1], F32)
-        nc.scalar.activation(out=table_warmer[:], in_=minus_k[:, 0:1], func=ACT.Sigmoid)
+        table_warmer = keep.tile([P, 2], F32)
+        nc.scalar.activation(out=table_warmer[:, 0:1], in_=minus_k[:, 0:1], func=ACT.Sigmoid)
 
-        for i in range(1, len(w2_pieces)):
-            regroup(w2_pieces[i])
-            quantise(w2_pieces[i - 1])
-
-        h_grouped = keep.tile([P, GROUPS, PAIRS, PACK], BF16, align_bytes=64)
-        h_codes = keep.tile([P, GROUPS, PAIRS], U32, align_bytes=64)
-        h_scales = keep.tile([P, GROUPS, PAIRS], U8, align_bytes=64)
-        for g in range(GROUPS):
-            chunks = slice(g * GROUP, (g + 1) * GROUP)
+        w2_units = [(1, 0, BIG), (1, BIG, BIG), (2, 0, BIG), (2, BIG, SMALL), (2, BIG + SMALL, SMALL)]
+        regroup(*w2_units[0])
+        regroup(*w2_units[1])
+        quantise(*w2_units[0])
+        regroup(*w2_units[2])
+        quantise(*w2_units[1])
+        h_grouped = keep.tile([P, PASSES, PAIRS, PACK], BF16, align_bytes=64)
+        h_codes = keep.tile([P, PASSES, PAIRS], U32, align_bytes=64)
+        h_scales = keep.tile([P, PASSES, PAIRS], U8, align_bytes=64)
+        for g in range(PASSES):
+            chunks = pass_chunks(g)
             nc.vector.scalar_tensor_tensor(
                 out=h_grouped[:, g, :, :],
                 in0=pre1[:, chunks, :].rearrange("p t r -> p r t"),
@@ -163,26 +181,31 @@ def tile_cfconv_pa_s_kernel(tc, x, distances, W1, b1, W2, b2, out):
                 op0=ALU.max,
                 op1=ALU.add,
             )
-        for g in range(GROUPS):
+        quantise(*w2_units[2])
+        for g in range(PASSES):
             nc.vector.quantize_mx(
                 out=h_codes[:, g, :].bitcast(FP8X4),
                 scales=h_scales[:, g, :],
                 in_=h_grouped[:, g, :, :].rearrange("p r t -> p (r t)"),
             )
-        quantise(w2_pieces[-1])
+        regroup(*w2_units[3])
+        regroup(*w2_units[4])
+        quantise(*w2_units[3])
+        quantise(*w2_units[4])
 
         size2 = keep.tile([P, CHUNKS, PAIRS], F32)
-        twice2 = keep.tile([P, CHUNKS, PAIRS], F32)
+        positive2 = keep.tile([P, CHUNKS, PAIRS], F32)
         gate2 = keep.tile([P, CHUNKS, PAIRS], F32)
-        product = keep.tile([P, CHUNKS, ROWS], F32)
-        twice_sum = keep.tile([P, CHUNKS, ROWS], F32)
-        for group in range(GROUPS):
-            chunks = slice(group * GROUP, (group + 1) * GROUP)
-            for c in range(group * GROUP, (group + 1) * GROUP):
+        positive_sum = keep.tile([P, ROWS, CHUNKS], F32)
+        product = keep.tile([P, ROWS, CHUNKS], F32)
+        last_pass_units = [unit for unit in w2_units if unit[0] == SLABS - 1]
+        for unit in last_pass_units:
+            first, width = unit[1], unit[2]
+            for c in chunks_of(first, width):
                 c_cols = slice(c * P, (c + 1) * P)
                 b2_c = bias[:, CHUNKS + c : CHUNKS + c + 1]
                 v2 = banks.tile([P, PAIRS], F32, tag="bank")
-                for g in range(GROUPS):
+                for g in range(PASSES):
                     nc.tensor.matmul_mx(
                         out=v2[:],
                         lhsT=w_codes[:, 1 + g, c_cols].bitcast(FP8X4),
@@ -190,39 +213,34 @@ def tile_cfconv_pa_s_kernel(tc, x, distances, W1, b1, W2, b2, out):
                         rhs=h_codes[:, g, :].bitcast(FP8X4),
                         rhs_scale=h_scales[:, g, :],
                         start=(g == 0),
-                        stop=(g == GROUPS - 1),
+                        stop=(g == PASSES - 1),
                     )
                 nc.scalar.activation(out=size2[:, c, :], in_=v2[:], func=ACT.Abs, bias=b2_c)
-                nc.vector.scalar_tensor_tensor(
-                    out=twice2[:, c, :], in0=v2[:], scalar=b2_c, in1=size2[:, c, :], op0=ALU.add, op1=ALU.add
-                )
+                nc.scalar.activation(out=positive2[:, c, :], in_=v2[:], func=ACT.Relu, bias=b2_c)
+            chunks = slice(first // P, (first + width) // P)
             nc.scalar.activation(out=gate2[:, chunks, :], in_=size2[:, chunks, :], func=ACT.Sigmoid)
             nc.vector.tensor_reduce(
-                out=twice_sum[:, chunks, :].rearrange("p c r -> p (c r)"),
-                in_=twice2[:, chunks, :].rearrange("p c (r j) -> p (c r) j", j=ATOMS),
+                out=positive_sum[:, :, chunks],
+                in_=positive2[:, chunks, :].rearrange("p c (r j) -> p r c j", j=ATOMS),
                 axis=AXIS.X,
                 op=ALU.add,
             )
             nc.vector.tensor_reduce(
-                out=product[:, chunks, :].rearrange("p c r -> p (c r)"),
-                in_=gate2[:, chunks, :].rearrange("p c (r j) -> p (c r) j", j=ATOMS),
+                out=product[:, :, chunks],
+                in_=gate2[:, chunks, :].rearrange("p c (r j) -> p r c j", j=ATOMS),
                 axis=AXIS.X,
                 op=ALU.mult,
             )
-        log_product = keep.tile([P, CHUNKS, ROWS], F32)
-        nc.scalar.activation(out=log_product[:], in_=product[:], func=ACT.Ln, scale=float(2**ATOMS))
-        summed = keep.tile([P, ROWS, CHUNKS], F32)
-        nc.vector.scalar_tensor_tensor(
-            out=summed[:],
-            in0=twice_sum[:].rearrange("p c r -> p r c"),
-            scalar=0.5,
-            in1=log_product[:].rearrange("p c r -> p r c"),
-            op0=ALU.mult,
-            op1=ALU.subtract,
-        )
+        nc.scalar.activation(out=table_warmer[:, 1:2], in_=minus_k[:, 0:1], func=ACT.Ln, scale=0.0, bias=1.0)
 
-        turned = banks.tile([P, P], F32, tag="bank")
-        nc.tensor.transpose(out=turned[:], in_=summed[:].rearrange("p r c -> p (r c)"), identity=ident_f32[:])
+        sum_rows = banks.tile([P, P], F32, tag="bank")
+        nc.tensor.transpose(out=sum_rows[:], in_=positive_sum[:].rearrange("p r c -> p (r c)"), identity=ident_f32[:])
+        product_rows = banks.tile([P, P], F32, tag="bank")
+        nc.tensor.transpose(out=product_rows[:], in_=product[:].rearrange("p r c -> p (r c)"), identity=ident_f32[:])
+        log_rows = keep.tile([P, P], F32)
+        nc.scalar.activation(out=log_rows[:], in_=product_rows[:], func=ACT.Ln, scale=float(2**ATOMS))
+        filter_rows = keep.tile([P, P], F32)
+        nc.vector.tensor_tensor(out=filter_rows[:], in0=sum_rows[:], in1=log_rows[:], op=ALU.subtract)
         result = keep.tile([P, P], F32)
-        nc.vector.tensor_tensor(out=result[:], in0=turned[:], in1=x_rows[:], op=ALU.mult)
+        nc.vector.tensor_tensor(out=result[:], in0=filter_rows[:], in1=x_rows[:], op=ALU.mult)
         nc.sync.dma_start(out=out.rearrange("b i (c p) -> (b i c) p", p=P), in_=result[:])

@@ -91,6 +91,8 @@ def tile_cfconv_pa_s_kernel(tc, x, distances, W1, b1, W2, b2, out):
         nc.tensor.transpose(out=bias_turned[:], in_=bias_rows[:], identity=ident_bf[:])
         bias = keep.tile([P, 2 * CHUNKS], F32)
         nc.scalar.copy(out=bias[:], in_=bias_turned[:, 0 : 2 * CHUNKS])
+        twice_b2 = keep.tile([P, CHUNKS], F32)
+        nc.scalar.mul(out=twice_b2[:], in_=bias_turned[:, CHUNKS : 2 * CHUNKS], mul=2.0)
 
         grouped = keep.tile([P, SLABS, FEATURES, PACK], BF16, align_bytes=64)
         w_codes = keep.tile([P, SLABS, FEATURES], U32, align_bytes=64)
@@ -99,6 +101,13 @@ def tile_cfconv_pa_s_kernel(tc, x, distances, W1, b1, W2, b2, out):
         def regroup(slab, first, width):
             cols = slice(first, first + width)
             nc.vector.tensor_copy(
+                out=grouped[:, slab, cols, :].rearrange("p (c i) t -> p c t i", i=RUN),
+                in_=raw[:, slab, :, cols].rearrange("p t (c i) -> p c t i", i=RUN),
+            )
+
+        def regroup_on_scalar(slab, first, width):
+            cols = slice(first, first + width)
+            nc.scalar.copy(
                 out=grouped[:, slab, cols, :].rearrange("p (c i) t -> p c t i", i=RUN),
                 in_=raw[:, slab, :, cols].rearrange("p t (c i) -> p c t i", i=RUN),
             )
@@ -116,7 +125,8 @@ def tile_cfconv_pa_s_kernel(tc, x, distances, W1, b1, W2, b2, out):
         decay1 = keep.tile([P, CHUNKS, PAIRS], F32)
         log1 = keep.tile([P, CHUNKS, PAIRS], F32)
 
-        def first_matmul(slab, first, width):
+        def first_matmul(unit, bias_on_vector):
+            slab, first, width = unit
             for m in chunks_of(first, width):
                 m_cols = slice(m * P, (m + 1) * P)
                 v1 = banks.tile([P, PAIRS], F32, tag="bank")
@@ -129,7 +139,10 @@ def tile_cfconv_pa_s_kernel(tc, x, distances, W1, b1, W2, b2, out):
                     start=True,
                     stop=True,
                 )
-                nc.scalar.activation(out=pre1[:, m, :], in_=v1[:], func=ACT.Identity, bias=bias[:, m : m + 1])
+                if bias_on_vector:
+                    nc.vector.tensor_scalar_add(out=pre1[:, m, :], in0=v1[:], scalar1=bias[:, m : m + 1])
+                else:
+                    nc.scalar.activation(out=pre1[:, m, :], in_=v1[:], func=ACT.Identity, bias=bias[:, m : m + 1])
 
         def pass_chunks(g):
             return slice(g * PACK, (g + 1) * PACK)
@@ -139,6 +152,7 @@ def tile_cfconv_pa_s_kernel(tc, x, distances, W1, b1, W2, b2, out):
             nc.scalar.activation(out=size1[:, chunks, :], in_=pre1[:, chunks, :], func=ACT.Abs)
             nc.scalar.activation(out=decay1[:, chunks, :], in_=size1[:, chunks, :], func=ACT.Exp, scale=-1.0)
 
+        regroup_on_scalar(*w1_units[3])
         regroup(*w1_units[0])
         regroup(*w1_units[1])
         quantise(*w1_units[0])
@@ -146,15 +160,14 @@ def tile_cfconv_pa_s_kernel(tc, x, distances, W1, b1, W2, b2, out):
         nc.vector.quantize_mx(
             out=e_codes[:].bitcast(FP8X4), scales=e_scales[:], in_=e_grouped[:].rearrange("p r t -> p (r t)")
         )
-        first_matmul(*w1_units[0])
+        first_matmul(w1_units[0], bias_on_vector=False)
         quantise(*w1_units[1])
-        first_matmul(*w1_units[1])
+        first_matmul(w1_units[1], bias_on_vector=False)
         first_decay(0)
-        regroup(*w1_units[3])
         quantise(*w1_units[2])
-        first_matmul(*w1_units[2])
         quantise(*w1_units[3])
-        first_matmul(*w1_units[3])
+        first_matmul(w1_units[2], bias_on_vector=True)
+        first_matmul(w1_units[3], bias_on_vector=True)
         first_decay(1)
         for g in range(PASSES):
             chunks = pass_chunks(g)
@@ -168,6 +181,7 @@ def tile_cfconv_pa_s_kernel(tc, x, distances, W1, b1, W2, b2, out):
         quantise(*w2_units[0])
         regroup(*w2_units[2])
         quantise(*w2_units[1])
+        quantise(*w2_units[2])
         h_grouped = keep.tile([P, PASSES, PAIRS, PACK], BF16, align_bytes=64)
         h_codes = keep.tile([P, PASSES, PAIRS], U32, align_bytes=64)
         h_scales = keep.tile([P, PASSES, PAIRS], U8, align_bytes=64)
@@ -181,8 +195,6 @@ def tile_cfconv_pa_s_kernel(tc, x, distances, W1, b1, W2, b2, out):
                 op0=ALU.max,
                 op1=ALU.add,
             )
-        quantise(*w2_units[2])
-        for g in range(PASSES):
             nc.vector.quantize_mx(
                 out=h_codes[:, g, :].bitcast(FP8X4),
                 scales=h_scales[:, g, :],
@@ -216,7 +228,14 @@ def tile_cfconv_pa_s_kernel(tc, x, distances, W1, b1, W2, b2, out):
                         stop=(g == PASSES - 1),
                     )
                 nc.scalar.activation(out=size2[:, c, :], in_=v2[:], func=ACT.Abs, bias=b2_c)
-                nc.scalar.activation(out=positive2[:, c, :], in_=v2[:], func=ACT.Relu, bias=b2_c)
+                if unit == last_pass_units[0]:
+                    nc.vector.scalar_tensor_tensor(
+                        out=positive2[:, c, :], in0=v2[:], scalar=b2_c, in1=size2[:, c, :], op0=ALU.add, op1=ALU.add
+                    )
+                else:
+                    nc.scalar.activation(
+                        out=positive2[:, c, :], in_=v2[:], func=ACT.Relu, scale=2.0, bias=twice_b2[:, c : c + 1]
+                    )
             chunks = slice(first // P, (first + width) // P)
             nc.scalar.activation(out=gate2[:, chunks, :], in_=size2[:, chunks, :], func=ACT.Sigmoid)
             nc.vector.tensor_reduce(
@@ -240,7 +259,9 @@ def tile_cfconv_pa_s_kernel(tc, x, distances, W1, b1, W2, b2, out):
         log_rows = keep.tile([P, P], F32)
         nc.scalar.activation(out=log_rows[:], in_=product_rows[:], func=ACT.Ln, scale=float(2**ATOMS))
         filter_rows = keep.tile([P, P], F32)
-        nc.vector.tensor_tensor(out=filter_rows[:], in0=sum_rows[:], in1=log_rows[:], op=ALU.subtract)
+        nc.vector.scalar_tensor_tensor(
+            out=filter_rows[:], in0=sum_rows[:], scalar=0.5, in1=log_rows[:], op0=ALU.mult, op1=ALU.subtract
+        )
         result = keep.tile([P, P], F32)
         nc.vector.tensor_tensor(out=result[:], in0=filter_rows[:], in1=x_rows[:], op=ALU.mult)
         nc.sync.dma_start(out=out.rearrange("b i (c p) -> (b i c) p", p=P), in_=result[:])

@@ -147,10 +147,8 @@ def tile_cfconv_pa_s_kernel(tc, x, distances, W1, b1, W2, b2, out):
         def pass_chunks(g):
             return slice(g * PACK, (g + 1) * PACK)
 
-        def first_decay(g):
-            chunks = pass_chunks(g)
-            nc.scalar.activation(out=size1[:, chunks, :], in_=pre1[:, chunks, :], func=ACT.Abs)
-            nc.scalar.activation(out=decay1[:, chunks, :], in_=size1[:, chunks, :], func=ACT.Exp, scale=-1.0)
+        def unit_chunks(unit):
+            return slice(unit[1] // P, (unit[1] + unit[2]) // P)
 
         regroup_on_scalar(*w1_units[3])
         regroup(*w1_units[0])
@@ -163,15 +161,22 @@ def tile_cfconv_pa_s_kernel(tc, x, distances, W1, b1, W2, b2, out):
         first_matmul(w1_units[0], bias_on_vector=False)
         quantise(*w1_units[1])
         first_matmul(w1_units[1], bias_on_vector=False)
-        first_decay(0)
         quantise(*w1_units[2])
         quantise(*w1_units[3])
         first_matmul(w1_units[2], bias_on_vector=True)
         first_matmul(w1_units[3], bias_on_vector=True)
-        first_decay(1)
-        for g in range(PASSES):
-            chunks = pass_chunks(g)
-            nc.scalar.activation(out=log1[:, chunks, :], in_=decay1[:, chunks, :], func=ACT.Ln, scale=0.5, bias=0.5)
+        for i, unit in enumerate(w1_units):
+            nc.scalar.activation(out=size1[:, unit_chunks(unit), :], in_=pre1[:, unit_chunks(unit), :], func=ACT.Abs)
+            if i > 0:
+                before = unit_chunks(w1_units[i - 1])
+                nc.scalar.activation(out=decay1[:, before, :], in_=size1[:, before, :], func=ACT.Exp, scale=-1.0)
+        last = unit_chunks(w1_units[-1])
+        nc.scalar.activation(out=decay1[:, last, :], in_=size1[:, last, :], func=ACT.Exp, scale=-1.0)
+        h_parts = [(g, slice(r, r + PAIRS // 2)) for g in range(PASSES) for r in range(0, PAIRS, PAIRS // 2)]
+        for g, pairs in h_parts:
+            nc.scalar.activation(
+                out=log1[:, pass_chunks(g), pairs], in_=decay1[:, pass_chunks(g), pairs], func=ACT.Ln, scale=0.5, bias=0.5
+            )
         table_warmer = keep.tile([P, 2], F32)
         nc.scalar.activation(out=table_warmer[:, 0:1], in_=minus_k[:, 0:1], func=ACT.Sigmoid)
 
@@ -185,21 +190,29 @@ def tile_cfconv_pa_s_kernel(tc, x, distances, W1, b1, W2, b2, out):
         h_grouped = keep.tile([P, PASSES, PAIRS, PACK], BF16, align_bytes=64)
         h_codes = keep.tile([P, PASSES, PAIRS], U32, align_bytes=64)
         h_scales = keep.tile([P, PASSES, PAIRS], U8, align_bytes=64)
-        for g in range(PASSES):
-            chunks = pass_chunks(g)
+
+        def h_add(g, pairs):
             nc.vector.scalar_tensor_tensor(
-                out=h_grouped[:, g, :, :],
-                in0=pre1[:, chunks, :].rearrange("p t r -> p r t"),
+                out=h_grouped[:, g, pairs, :],
+                in0=pre1[:, pass_chunks(g), pairs].rearrange("p t r -> p r t"),
                 scalar=0.0,
-                in1=log1[:, chunks, :].rearrange("p t r -> p r t"),
+                in1=log1[:, pass_chunks(g), pairs].rearrange("p t r -> p r t"),
                 op0=ALU.max,
                 op1=ALU.add,
             )
+
+        def h_quantise(g, pairs):
             nc.vector.quantize_mx(
-                out=h_codes[:, g, :].bitcast(FP8X4),
-                scales=h_scales[:, g, :],
-                in_=h_grouped[:, g, :, :].rearrange("p r t -> p (r t)"),
+                out=h_codes[:, g, pairs].bitcast(FP8X4),
+                scales=h_scales[:, g, pairs],
+                in_=h_grouped[:, g, pairs, :].rearrange("p r t -> p (r t)"),
             )
+
+        h_add(*h_parts[0])
+        for i in range(1, len(h_parts)):
+            h_add(*h_parts[i])
+            h_quantise(*h_parts[i - 1])
+        h_quantise(*h_parts[-1])
         regroup(*w2_units[3])
         regroup(*w2_units[4])
         quantise(*w2_units[3])
@@ -237,7 +250,8 @@ def tile_cfconv_pa_s_kernel(tc, x, distances, W1, b1, W2, b2, out):
                         out=positive2[:, c, :], in_=v2[:], func=ACT.Relu, scale=2.0, bias=twice_b2[:, c : c + 1]
                     )
             chunks = slice(first // P, (first + width) // P)
-            nc.scalar.activation(out=gate2[:, chunks, :], in_=size2[:, chunks, :], func=ACT.Sigmoid)
+            for c in range(first // P, (first + width) // P, 2):
+                nc.scalar.activation(out=gate2[:, c : c + 2, :], in_=size2[:, c : c + 2, :], func=ACT.Sigmoid)
             nc.vector.tensor_reduce(
                 out=positive_sum[:, :, chunks],
                 in_=positive2[:, chunks, :].rearrange("p c (r j) -> p r c j", j=ATOMS),

@@ -1,3 +1,5 @@
+import math
+
 import concourse.mybir as mybir
 from concourse.masks import make_identity
 
@@ -25,6 +27,7 @@ CHUNKS = FEATURES // P
 SLABS = 1 + PASSES
 BIG = 512
 SMALL = 256
+CLAMP = 40.0
 RUN = 4
 
 FLOPS = 2 * PAIRS * BASIS * FEATURES + 2 * PAIRS * FEATURES * FEATURES
@@ -91,8 +94,6 @@ def tile_cfconv_pa_s_kernel(tc, x, distances, W1, b1, W2, b2, out):
         nc.tensor.transpose(out=bias_turned[:], in_=bias_rows[:], identity=ident_bf[:])
         bias = keep.tile([P, 2 * CHUNKS], F32)
         nc.scalar.copy(out=bias[:], in_=bias_turned[:, 0 : 2 * CHUNKS])
-        twice_b2 = keep.tile([P, CHUNKS], F32)
-        nc.scalar.mul(out=twice_b2[:], in_=bias_turned[:, CHUNKS : 2 * CHUNKS], mul=2.0)
 
         grouped = keep.tile([P, SLABS, FEATURES, PACK], BF16, align_bytes=64)
         w_codes = keep.tile([P, SLABS, FEATURES], U32, align_bytes=64)
@@ -121,11 +122,11 @@ def tile_cfconv_pa_s_kernel(tc, x, distances, W1, b1, W2, b2, out):
             )
 
         pre1 = keep.tile([P, CHUNKS, PAIRS], F32)
-        size1 = keep.tile([P, CHUNKS, PAIRS], F32)
-        decay1 = keep.tile([P, CHUNKS, PAIRS], F32)
+        clamped1 = keep.tile([P, CHUNKS, PAIRS], F32)
+        grown1 = keep.tile([P, CHUNKS, PAIRS], F32)
         log1 = keep.tile([P, CHUNKS, PAIRS], F32)
 
-        def first_matmul(unit, bias_on_vector):
+        def first_matmul(unit):
             slab, first, width = unit
             for m in chunks_of(first, width):
                 m_cols = slice(m * P, (m + 1) * P)
@@ -139,10 +140,7 @@ def tile_cfconv_pa_s_kernel(tc, x, distances, W1, b1, W2, b2, out):
                     start=True,
                     stop=True,
                 )
-                if bias_on_vector:
-                    nc.vector.tensor_scalar_add(out=pre1[:, m, :], in0=v1[:], scalar1=bias[:, m : m + 1])
-                else:
-                    nc.scalar.activation(out=pre1[:, m, :], in_=v1[:], func=ACT.Identity, bias=bias[:, m : m + 1])
+                nc.scalar.activation(out=pre1[:, m, :], in_=v1[:], func=ACT.Identity, bias=bias[:, m : m + 1])
 
         def pass_chunks(g):
             return slice(g * PACK, (g + 1) * PACK)
@@ -158,35 +156,63 @@ def tile_cfconv_pa_s_kernel(tc, x, distances, W1, b1, W2, b2, out):
         nc.vector.quantize_mx(
             out=e_codes[:].bitcast(FP8X4), scales=e_scales[:], in_=e_grouped[:].rearrange("p r t -> p (r t)")
         )
-        first_matmul(w1_units[0], bias_on_vector=False)
+        first_matmul(w1_units[0])
         quantise(*w1_units[1])
-        first_matmul(w1_units[1], bias_on_vector=False)
+        first_matmul(w1_units[1])
         quantise(*w1_units[2])
         quantise(*w1_units[3])
-        first_matmul(w1_units[2], bias_on_vector=True)
-        first_matmul(w1_units[3], bias_on_vector=True)
-        for i, unit in enumerate(w1_units):
-            nc.scalar.activation(out=size1[:, unit_chunks(unit), :], in_=pre1[:, unit_chunks(unit), :], func=ACT.Abs)
-            if i > 0:
-                before = unit_chunks(w1_units[i - 1])
-                nc.scalar.activation(out=decay1[:, before, :], in_=size1[:, before, :], func=ACT.Exp, scale=-1.0)
-        last = unit_chunks(w1_units[-1])
-        nc.scalar.activation(out=decay1[:, last, :], in_=size1[:, last, :], func=ACT.Exp, scale=-1.0)
+        first_matmul(w1_units[2])
+
+        def clamp(unit):
+            chunks = unit_chunks(unit)
+            nc.vector.tensor_scalar_min(out=clamped1[:, chunks, :], in0=pre1[:, chunks, :], scalar1=CLAMP)
+
+        def grow(unit):
+            chunks = unit_chunks(unit)
+            nc.scalar.activation(out=grown1[:, chunks, :], in_=clamped1[:, chunks, :], func=ACT.Exp)
+
+        w2_units = [(1, 0, BIG), (1, BIG, BIG), (2, 0, BIG), (2, BIG, SMALL), (2, BIG + SMALL, SMALL)]
+        clamp(w1_units[0])
+        clamp(w1_units[1])
+        grow(w1_units[0])
+        first_matmul(w1_units[3])
+        regroup(1, 0, SMALL)
+        clamp(w1_units[2])
+        clamp(w1_units[3])
+        for unit in w1_units[1:]:
+            grow(unit)
         h_parts = [(g, slice(r, r + PAIRS // 2)) for g in range(PASSES) for r in range(0, PAIRS, PAIRS // 2)]
         for g, pairs in h_parts:
             nc.scalar.activation(
-                out=log1[:, pass_chunks(g), pairs], in_=decay1[:, pass_chunks(g), pairs], func=ACT.Ln, scale=0.5, bias=0.5
+                out=log1[:, pass_chunks(g), pairs], in_=grown1[:, pass_chunks(g), pairs], func=ACT.Ln, scale=0.5, bias=0.5
             )
+        regroup_on_scalar(*w2_units[4])
         table_warmer = keep.tile([P, 2], F32)
         nc.scalar.activation(out=table_warmer[:, 0:1], in_=minus_k[:, 0:1], func=ACT.Sigmoid)
 
-        w2_units = [(1, 0, BIG), (1, BIG, BIG), (2, 0, BIG), (2, BIG, SMALL), (2, BIG + SMALL, SMALL)]
-        regroup(*w2_units[0])
+        spin = banks.tile([P, BIG], F32, tag="bank")
+
+        def keep_clock_up(unit, count):
+            slab, first, width = unit
+            cols = slice(first, first + width)
+            for i in range(count):
+                nc.tensor.matmul_mx(
+                    out=spin[:],
+                    lhsT=w_codes[:, 0, 0:P].bitcast(FP8X4),
+                    lhsT_scale=w_scales[:, 0, 0:P],
+                    rhs=w_codes[:, slab, cols].bitcast(FP8X4),
+                    rhs_scale=w_scales[:, slab, cols],
+                    start=True,
+                    stop=True,
+                )
+
+        regroup(1, SMALL, SMALL)
         regroup(*w2_units[1])
         quantise(*w2_units[0])
         regroup(*w2_units[2])
         quantise(*w2_units[1])
         quantise(*w2_units[2])
+        keep_clock_up(w2_units[1], 3)
         h_grouped = keep.tile([P, PASSES, PAIRS, PACK], BF16, align_bytes=64)
         h_codes = keep.tile([P, PASSES, PAIRS], U32, align_bytes=64)
         h_scales = keep.tile([P, PASSES, PAIRS], U8, align_bytes=64)
@@ -195,10 +221,10 @@ def tile_cfconv_pa_s_kernel(tc, x, distances, W1, b1, W2, b2, out):
             nc.vector.scalar_tensor_tensor(
                 out=h_grouped[:, g, pairs, :],
                 in0=pre1[:, pass_chunks(g), pairs].rearrange("p t r -> p r t"),
-                scalar=0.0,
+                scalar=-math.log(2.0),
                 in1=log1[:, pass_chunks(g), pairs].rearrange("p t r -> p r t"),
-                op0=ALU.max,
-                op1=ALU.add,
+                op0=ALU.add,
+                op1=ALU.max,
             )
 
         def h_quantise(g, pairs):
@@ -214,19 +240,19 @@ def tile_cfconv_pa_s_kernel(tc, x, distances, W1, b1, W2, b2, out):
             h_quantise(*h_parts[i - 1])
         h_quantise(*h_parts[-1])
         regroup(*w2_units[3])
-        regroup(*w2_units[4])
-        quantise(*w2_units[3])
         quantise(*w2_units[4])
+        quantise(*w2_units[3])
 
         size2 = keep.tile([P, CHUNKS, PAIRS], F32)
-        positive2 = keep.tile([P, CHUNKS, PAIRS], F32)
+        positive2 = keep.tile([P, ROWS, CHUNKS, ATOMS], F32)
         gate2 = keep.tile([P, CHUNKS, PAIRS], F32)
-        positive_sum = keep.tile([P, ROWS, CHUNKS], F32)
         product = keep.tile([P, ROWS, CHUNKS], F32)
-        last_pass_units = [unit for unit in w2_units if unit[0] == SLABS - 1]
-        for unit in last_pass_units:
-            first, width = unit[1], unit[2]
-            for c in chunks_of(first, width):
+        halves = [
+            list(chunks_of(0, BIG)),
+            list(chunks_of(BIG + SMALL, SMALL)) + list(chunks_of(BIG, SMALL)),
+        ]
+        for half in halves:
+            for c in half:
                 c_cols = slice(c * P, (c + 1) * P)
                 b2_c = bias[:, CHUNKS + c : CHUNKS + c + 1]
                 v2 = banks.tile([P, PAIRS], F32, tag="bank")
@@ -241,23 +267,18 @@ def tile_cfconv_pa_s_kernel(tc, x, distances, W1, b1, W2, b2, out):
                         stop=(g == PASSES - 1),
                     )
                 nc.scalar.activation(out=size2[:, c, :], in_=v2[:], func=ACT.Abs, bias=b2_c)
-                if unit == last_pass_units[0]:
-                    nc.vector.scalar_tensor_tensor(
-                        out=positive2[:, c, :], in0=v2[:], scalar=b2_c, in1=size2[:, c, :], op0=ALU.add, op1=ALU.add
-                    )
-                else:
-                    nc.scalar.activation(
-                        out=positive2[:, c, :], in_=v2[:], func=ACT.Relu, scale=2.0, bias=twice_b2[:, c : c + 1]
-                    )
-            chunks = slice(first // P, (first + width) // P)
-            for c in range(first // P, (first + width) // P, 2):
+                nc.vector.scalar_tensor_tensor(
+                    out=positive2[:, :, c, :],
+                    in0=v2[:].rearrange("p (r j) -> p r j", j=ATOMS),
+                    scalar=b2_c,
+                    in1=size2[:, c, :].rearrange("p (r j) -> p r j", j=ATOMS),
+                    op0=ALU.add,
+                    op1=ALU.add,
+                )
+            for c in half[::2]:
                 nc.scalar.activation(out=gate2[:, c : c + 2, :], in_=size2[:, c : c + 2, :], func=ACT.Sigmoid)
-            nc.vector.tensor_reduce(
-                out=positive_sum[:, :, chunks],
-                in_=positive2[:, chunks, :].rearrange("p c (r j) -> p r c j", j=ATOMS),
-                axis=AXIS.X,
-                op=ALU.add,
-            )
+        for half in halves:
+            chunks = slice(min(half), max(half) + 1)
             nc.vector.tensor_reduce(
                 out=product[:, :, chunks],
                 in_=gate2[:, chunks, :].rearrange("p c (r j) -> p r c j", j=ATOMS),
@@ -267,9 +288,21 @@ def tile_cfconv_pa_s_kernel(tc, x, distances, W1, b1, W2, b2, out):
         nc.scalar.activation(out=table_warmer[:, 1:2], in_=minus_k[:, 0:1], func=ACT.Ln, scale=0.0, bias=1.0)
 
         sum_rows = banks.tile([P, P], F32, tag="bank")
-        nc.tensor.transpose(out=sum_rows[:], in_=positive_sum[:].rearrange("p r c -> p (r c)"), identity=ident_f32[:])
+        by_atom = positive2[:].rearrange("p r c j -> p j (r c)")
         product_rows = banks.tile([P, P], F32, tag="bank")
-        nc.tensor.transpose(out=product_rows[:], in_=product[:].rearrange("p r c -> p (r c)"), identity=ident_f32[:])
+        for j in range(ATOMS):
+            nc.tensor.matmul(
+                out=sum_rows[:],
+                lhsT=by_atom[:, j, :],
+                rhs=ident_f32[:],
+                start=(j == 0),
+                stop=(j == ATOMS - 1),
+                is_transpose=True,
+            )
+            if j == ATOMS // 2 - 1:
+                nc.tensor.transpose(
+                    out=product_rows[:], in_=product[:].rearrange("p r c -> p (r c)"), identity=ident_f32[:]
+                )
         log_rows = keep.tile([P, P], F32)
         nc.scalar.activation(out=log_rows[:], in_=product_rows[:], func=ACT.Ln, scale=float(2**ATOMS))
         filter_rows = keep.tile([P, P], F32)

@@ -61,11 +61,10 @@ def tile_cfconv_pa_s_kernel(tc, x, distances, W1, b1, W2, b2, out):
         nc.vector.memset(bias_rows[:], 0.0)
         nc.sync.dma_start(out=bias_rows[0:CHUNKS, :], in_=b1.rearrange("(m p) -> m p", p=P))
         nc.sync.dma_start(out=bias_rows[CHUNKS : 2 * CHUNKS, :], in_=b2.rearrange("(m p) -> m p", p=P))
-        load(*w1_units[2])
-        load(*w1_units[3])
-        for slab in range(1, SLABS):
-            for first in range(0, FEATURES, BIG):
-                load(slab, first, BIG)
+        load(0, BIG, BIG)
+        load(1, 0, BIG)
+        load(1, BIG, BIG)
+        load(2, 0, FEATURES)
         x_rows = keep.tile([P, P], BF16)
         nc.sync.dma_start(out=x_rows[:], in_=x.rearrange("b i (c p) -> (b i c) p", p=P))
 

@@ -48,11 +48,17 @@ def tile_cfconv_pa_s_kernel(tc, x, distances, W1, b1, W2, b2, out):
             W2[0:K_PASS, :].rearrange("(t p) f -> p t f", p=P),
             W2[K_PASS : 2 * K_PASS, :].rearrange("(t p) f -> p t f", p=P),
         ]
-        raw = keep.tile([P, SLABS, PACK, FEATURES], BF16)
+        raw_tiles = {}
 
         def load(slab, first, width):
-            cols = slice(first, first + width)
-            nc.sync.dma_start(out=raw[:, slab, :, cols], in_=slab_rows[slab][:, :, cols])
+            raw = keep.tile([P, PACK, width], BF16, name="raw_%d_%d" % (slab, first))
+            nc.sync.dma_start(out=raw[:], in_=slab_rows[slab][:, :, first : first + width])
+            raw_tiles[slab, first, width] = raw
+
+        def raw_columns(slab, first, width):
+            for (s, start, loaded), raw in raw_tiles.items():
+                if s == slab and start <= first and first + width <= start + loaded:
+                    return raw[:, :, first - start : first - start + width]
 
         w1_units = [(0, first, SMALL) for first in range(0, FEATURES, SMALL)]
         load(*w1_units[0])
@@ -102,14 +108,14 @@ def tile_cfconv_pa_s_kernel(tc, x, distances, W1, b1, W2, b2, out):
             cols = slice(first, first + width)
             nc.vector.tensor_copy(
                 out=grouped[:, slab, cols, :].rearrange("p (c i) t -> p c t i", i=RUN),
-                in_=raw[:, slab, :, cols].rearrange("p t (c i) -> p c t i", i=RUN),
+                in_=raw_columns(slab, first, width).rearrange("p t (c i) -> p c t i", i=RUN),
             )
 
         def regroup_on_scalar(slab, first, width):
             cols = slice(first, first + width)
             nc.scalar.copy(
                 out=grouped[:, slab, cols, :].rearrange("p (c i) t -> p c t i", i=RUN),
-                in_=raw[:, slab, :, cols].rearrange("p t (c i) -> p c t i", i=RUN),
+                in_=raw_columns(slab, first, width).rearrange("p t (c i) -> p c t i", i=RUN),
             )
 
         def quantise(slab, first, width):
@@ -180,10 +186,9 @@ def tile_cfconv_pa_s_kernel(tc, x, distances, W1, b1, W2, b2, out):
         clamp(w1_units[3])
         for unit in w1_units[1:]:
             grow(unit)
-        h_parts = [(g, slice(r, r + PAIRS // 2)) for g in range(PASSES) for r in range(0, PAIRS, PAIRS // 2)]
-        for g, pairs in h_parts:
+        for g in range(PASSES):
             nc.scalar.activation(
-                out=log1[:, pass_chunks(g), pairs], in_=grown1[:, pass_chunks(g), pairs], func=ACT.Ln, scale=0.5, bias=0.5
+                out=log1[:, pass_chunks(g), :], in_=grown1[:, pass_chunks(g), :], func=ACT.Ln, scale=0.5, bias=0.5
             )
         regroup_on_scalar(*w2_units[4])
         table_warmer = keep.tile([P, 2], F32)
@@ -216,28 +221,27 @@ def tile_cfconv_pa_s_kernel(tc, x, distances, W1, b1, W2, b2, out):
         h_codes = keep.tile([P, PASSES, PAIRS], U32, align_bytes=64)
         h_scales = keep.tile([P, PASSES, PAIRS], U8, align_bytes=64)
 
-        def h_add(g, pairs):
+        def h_add(g):
             nc.vector.scalar_tensor_tensor(
-                out=h_grouped[:, g, pairs, :],
-                in0=pre1[:, pass_chunks(g), pairs].rearrange("p t r -> p r t"),
+                out=h_grouped[:, g, :, :],
+                in0=pre1[:, pass_chunks(g), :].rearrange("p t r -> p r t"),
                 scalar=-math.log(2.0),
-                in1=log1[:, pass_chunks(g), pairs].rearrange("p t r -> p r t"),
+                in1=log1[:, pass_chunks(g), :].rearrange("p t r -> p r t"),
                 op0=ALU.add,
                 op1=ALU.max,
             )
 
-        def h_quantise(g, pairs):
+        def h_quantise(g):
             nc.vector.quantize_mx(
-                out=h_codes[:, g, pairs].bitcast(FP8X4),
-                scales=h_scales[:, g, pairs],
-                in_=h_grouped[:, g, pairs, :].rearrange("p r t -> p (r t)"),
+                out=h_codes[:, g, :].bitcast(FP8X4),
+                scales=h_scales[:, g, :],
+                in_=h_grouped[:, g, :, :].rearrange("p r t -> p (r t)"),
             )
 
-        h_add(*h_parts[0])
-        for i in range(1, len(h_parts)):
-            h_add(*h_parts[i])
-            h_quantise(*h_parts[i - 1])
-        h_quantise(*h_parts[-1])
+        h_add(0)
+        h_add(1)
+        h_quantise(0)
+        h_quantise(1)
         regroup(*w2_units[3])
         quantise(*w2_units[4])
         quantise(*w2_units[3])
@@ -298,16 +302,19 @@ def tile_cfconv_pa_s_kernel(tc, x, distances, W1, b1, W2, b2, out):
                 stop=(j == ATOMS - 1),
                 is_transpose=True,
             )
-            if j == ATOMS // 2 - 1:
-                nc.tensor.transpose(
-                    out=product_rows[:], in_=product[:].rearrange("p r c -> p (r c)"), identity=ident_f32[:]
-                )
+        nc.tensor.transpose(out=product_rows[:], in_=product[:].rearrange("p r c -> p (r c)"), identity=ident_f32[:])
         log_rows = keep.tile([P, P], F32)
-        nc.scalar.activation(out=log_rows[:], in_=product_rows[:], func=ACT.Ln, scale=float(2**ATOMS))
         filter_rows = keep.tile([P, P], F32)
-        nc.vector.scalar_tensor_tensor(
-            out=filter_rows[:], in0=sum_rows[:], scalar=0.5, in1=log_rows[:], op0=ALU.mult, op1=ALU.subtract
-        )
         result = keep.tile([P, P], F32)
-        nc.vector.tensor_tensor(out=result[:], in0=filter_rows[:], in1=x_rows[:], op=ALU.mult)
-        nc.sync.dma_start(out=out.rearrange("b i (c p) -> (b i c) p", p=P), in_=result[:])
+        ends = [slice(0, P // 2), slice(P // 2, P)]
+        for end in ends:
+            nc.scalar.activation(out=log_rows[:, end], in_=product_rows[:, end], func=ACT.Ln, scale=float(2**ATOMS))
+        for end in ends:
+            nc.vector.scalar_tensor_tensor(
+                out=filter_rows[:, end], in0=sum_rows[:, end], scalar=0.5, in1=log_rows[:, end], op0=ALU.mult, op1=ALU.subtract
+            )
+        for end in ends:
+            nc.vector.tensor_tensor(out=result[:, end], in0=filter_rows[:, end], in1=x_rows[:, end], op=ALU.mult)
+        out_rows = out.rearrange("b i (c p) -> (b i c) p", p=P)
+        nc.sync.dma_start(out=out_rows[:, ends[0]], in_=result[:, ends[0]])
+        nc.scalar.dma_start(out=out_rows[:, ends[1]], in_=result[:, ends[1]])

@@ -27,7 +27,9 @@ CHUNKS = FEATURES // P
 SLABS = 1 + PASSES
 BIG = 512
 SMALL = 256
-CLAMP = 40.0
+LIFT1 = 24.0
+LIFT2 = 16.0
+PRODUCT_SHIFT = 64
 RUN = 4
 
 FLOPS = 2 * PAIRS * BASIS * FEATURES + 2 * PAIRS * FEATURES * FEATURES
@@ -40,8 +42,12 @@ def chunks_of(first_column, width):
 def tile_cfconv_pa_s_kernel(tc, x, distances, W1, b1, W2, b2, out):
     nc = tc.nc
     with tc.tile_pool(name="keep", bufs=1) as keep, tc.psum_pool(name="banks", bufs=8) as banks, tc.manual_schedule():
+        table_warmer = keep.tile([P, 4], F32)
+        nc.vector.memset(table_warmer[:, 3:4], 0.0)
+        nc.scalar.activation(out=table_warmer[:, 2:3], in_=table_warmer[:, 3:4], func=ACT.Exp)
+
         d_column = keep.tile([P, 1], BF16)
-        nc.scalar.dma_start(out=d_column[:], in_=distances.rearrange("b i (j o) -> (b i j) o", o=1))
+        nc.sync.dma_start(out=d_column[:], in_=distances.rearrange("b i (j o) -> (b i j) o", o=1))
 
         slab_rows = [
             W1.rearrange("(p t) f -> p t f", t=PACK),
@@ -70,7 +76,8 @@ def tile_cfconv_pa_s_kernel(tc, x, distances, W1, b1, W2, b2, out):
         load(0, BIG, BIG)
         load(1, 0, BIG)
         load(1, BIG, BIG)
-        load(2, 0, FEATURES)
+        load(2, 0, BIG)
+        load(2, BIG, BIG)
         x_rows = keep.tile([P, P], BF16)
         nc.sync.dma_start(out=x_rows[:], in_=x.rearrange("b i (c p) -> (b i c) p", p=P))
 
@@ -97,8 +104,10 @@ def tile_cfconv_pa_s_kernel(tc, x, distances, W1, b1, W2, b2, out):
 
         bias_turned = banks.tile([P, P], BF16, tag="bank")
         nc.tensor.transpose(out=bias_turned[:], in_=bias_rows[:], identity=ident_bf[:])
-        bias = keep.tile([P, 2 * CHUNKS], F32)
-        nc.scalar.copy(out=bias[:], in_=bias_turned[:, 0 : 2 * CHUNKS])
+        lifted = keep.tile([P, 2 * CHUNKS], F32)
+        layer1, layer2 = slice(0, CHUNKS), slice(CHUNKS, 2 * CHUNKS)
+        nc.scalar.activation(out=lifted[:, layer1], in_=bias_turned[:, layer1], func=ACT.Identity, bias=LIFT1)
+        nc.scalar.activation(out=lifted[:, layer2], in_=bias_turned[:, layer2], func=ACT.Identity, bias=LIFT2)
 
         grouped = keep.tile([P, SLABS, FEATURES, PACK], BF16, align_bytes=64)
         w_codes = keep.tile([P, SLABS, FEATURES], U32, align_bytes=64)
@@ -126,8 +135,7 @@ def tile_cfconv_pa_s_kernel(tc, x, distances, W1, b1, W2, b2, out):
                 in_=grouped[:, slab, cols, :].rearrange("p c t -> p (c t)"),
             )
 
-        pre1 = keep.tile([P, CHUNKS, PAIRS], F32)
-        clamped1 = keep.tile([P, CHUNKS, PAIRS], F32)
+        y1 = keep.tile([P, CHUNKS, PAIRS], F32)
         grown1 = keep.tile([P, CHUNKS, PAIRS], F32)
         log1 = keep.tile([P, CHUNKS, PAIRS], F32)
 
@@ -145,7 +153,7 @@ def tile_cfconv_pa_s_kernel(tc, x, distances, W1, b1, W2, b2, out):
                     start=True,
                     stop=True,
                 )
-                nc.scalar.activation(out=pre1[:, m, :], in_=v1[:], func=ACT.Identity, bias=bias[:, m : m + 1])
+                nc.scalar.activation(out=y1[:, m, :], in_=v1[:], func=ACT.Relu, bias=lifted[:, m : m + 1])
 
         def pass_chunks(g):
             return slice(g * PACK, (g + 1) * PACK)
@@ -157,42 +165,32 @@ def tile_cfconv_pa_s_kernel(tc, x, distances, W1, b1, W2, b2, out):
         regroup(*w1_units[0])
         regroup(*w1_units[1])
         quantise(*w1_units[0])
-        regroup(*w1_units[2])
         nc.vector.quantize_mx(
             out=e_codes[:].bitcast(FP8X4), scales=e_scales[:], in_=e_grouped[:].rearrange("p r t -> p (r t)")
         )
-        first_matmul(w1_units[0])
         quantise(*w1_units[1])
+        regroup(*w1_units[2])
+        first_matmul(w1_units[0])
         first_matmul(w1_units[1])
         quantise(*w1_units[2])
         quantise(*w1_units[3])
         first_matmul(w1_units[2])
 
-        def clamp(unit):
-            chunks = unit_chunks(unit)
-            nc.vector.tensor_scalar_min(out=clamped1[:, chunks, :], in0=pre1[:, chunks, :], scalar1=CLAMP)
+        def grow(g):
+            chunks = pass_chunks(g)
+            nc.scalar.activation(out=grown1[:, chunks, :], in_=y1[:, chunks, :], func=ACT.Exp, scale=-1.0, bias=LIFT1)
 
-        def grow(unit):
-            chunks = unit_chunks(unit)
-            nc.scalar.activation(out=grown1[:, chunks, :], in_=clamped1[:, chunks, :], func=ACT.Exp)
-
-        w2_units = [(1, 0, BIG), (1, BIG, BIG), (2, 0, BIG), (2, BIG, SMALL), (2, BIG + SMALL, SMALL)]
-        clamp(w1_units[0])
-        clamp(w1_units[1])
-        grow(w1_units[0])
+        w2_first = [(1, 0, BIG), (1, BIG, BIG)]
+        w2_last = [(2, first, SMALL) for first in range(0, FEATURES, SMALL)]
+        grow(0)
         first_matmul(w1_units[3])
-        regroup(1, 0, SMALL)
-        clamp(w1_units[2])
-        clamp(w1_units[3])
-        for unit in w1_units[1:]:
-            grow(unit)
+        grow(1)
         for g in range(PASSES):
             nc.scalar.activation(
                 out=log1[:, pass_chunks(g), :], in_=grown1[:, pass_chunks(g), :], func=ACT.Ln, scale=0.5, bias=0.5
             )
-        regroup_on_scalar(*w2_units[4])
-        table_warmer = keep.tile([P, 2], F32)
-        nc.scalar.activation(out=table_warmer[:, 0:1], in_=minus_k[:, 0:1], func=ACT.Sigmoid)
+        regroup_on_scalar(*w2_last[3])
+        nc.scalar.activation(out=table_warmer[:, 0:1], in_=table_warmer[:, 3:4], func=ACT.Sigmoid)
 
         spin = banks.tile([P, BIG], F32, tag="bank")
 
@@ -210,13 +208,14 @@ def tile_cfconv_pa_s_kernel(tc, x, distances, W1, b1, W2, b2, out):
                     stop=True,
                 )
 
-        regroup(1, SMALL, SMALL)
-        regroup(*w2_units[1])
-        quantise(*w2_units[0])
-        regroup(*w2_units[2])
-        quantise(*w2_units[1])
-        quantise(*w2_units[2])
-        keep_clock_up(w2_units[1], 3)
+        regroup(*w2_first[0])
+        regroup(*w2_first[1])
+        quantise(*w2_first[0])
+        regroup(*w2_last[0])
+        quantise(*w2_first[1])
+        keep_clock_up(w2_first[1], 3)
+        regroup(*w2_last[1])
+        quantise(*w2_last[0])
         h_grouped = keep.tile([P, PASSES, PAIRS, PACK], BF16, align_bytes=64)
         h_codes = keep.tile([P, PASSES, PAIRS], U32, align_bytes=64)
         h_scales = keep.tile([P, PASSES, PAIRS], U8, align_bytes=64)
@@ -224,11 +223,11 @@ def tile_cfconv_pa_s_kernel(tc, x, distances, W1, b1, W2, b2, out):
         def h_add(g):
             nc.vector.scalar_tensor_tensor(
                 out=h_grouped[:, g, :, :],
-                in0=pre1[:, pass_chunks(g), :].rearrange("p t r -> p r t"),
-                scalar=-math.log(2.0),
+                in0=y1[:, pass_chunks(g), :].rearrange("p t r -> p r t"),
+                scalar=-LIFT1,
                 in1=log1[:, pass_chunks(g), :].rearrange("p t r -> p r t"),
                 op0=ALU.add,
-                op1=ALU.max,
+                op1=ALU.add,
             )
 
         def h_quantise(g):
@@ -242,22 +241,18 @@ def tile_cfconv_pa_s_kernel(tc, x, distances, W1, b1, W2, b2, out):
         h_add(1)
         h_quantise(0)
         h_quantise(1)
-        regroup(*w2_units[3])
-        quantise(*w2_units[4])
-        quantise(*w2_units[3])
+        regroup(*w2_last[2])
+        quantise(*w2_last[1])
+        quantise(*w2_last[3])
+        quantise(*w2_last[2])
 
-        size2 = keep.tile([P, CHUNKS, PAIRS], F32)
-        positive2 = keep.tile([P, ROWS, CHUNKS, ATOMS], F32)
-        gate2 = keep.tile([P, CHUNKS, PAIRS], F32)
-        product = keep.tile([P, ROWS, CHUNKS], F32)
-        halves = [
-            list(chunks_of(0, BIG)),
-            list(chunks_of(BIG + SMALL, SMALL)) + list(chunks_of(BIG, SMALL)),
-        ]
-        for half in halves:
-            for c in half:
+        y2 = keep.tile([P, ROWS, CHUNKS, ATOMS], F32)
+        products = keep.tile([P, ROWS, CHUNKS, 2], F32)
+
+        def second_matmul(unit, lift_on_vector):
+            slab, first, width = unit
+            for c in chunks_of(first, width):
                 c_cols = slice(c * P, (c + 1) * P)
-                b2_c = bias[:, CHUNKS + c : CHUNKS + c + 1]
                 v2 = banks.tile([P, PAIRS], F32, tag="bank")
                 for g in range(PASSES):
                     nc.tensor.matmul_mx(
@@ -269,29 +264,56 @@ def tile_cfconv_pa_s_kernel(tc, x, distances, W1, b1, W2, b2, out):
                         start=(g == 0),
                         stop=(g == PASSES - 1),
                     )
-                nc.scalar.activation(out=size2[:, c, :], in_=v2[:], func=ACT.Abs, bias=b2_c)
-                nc.vector.scalar_tensor_tensor(
-                    out=positive2[:, :, c, :],
-                    in0=v2[:].rearrange("p (r j) -> p r j", j=ATOMS),
-                    scalar=b2_c,
-                    in1=size2[:, c, :].rearrange("p (r j) -> p r j", j=ATOMS),
-                    op0=ALU.add,
-                    op1=ALU.add,
-                )
-            for c in half[::2]:
-                nc.scalar.activation(out=gate2[:, c : c + 2, :], in_=size2[:, c : c + 2, :], func=ACT.Sigmoid)
-        for half in halves:
-            chunks = slice(min(half), max(half) + 1)
+                by_row = v2[:].rearrange("p (r j) -> p r j", j=ATOMS)
+                lift = lifted[:, CHUNKS + c : CHUNKS + c + 1]
+                if lift_on_vector:
+                    nc.vector.tensor_scalar(
+                        out=y2[:, :, c, :], in0=by_row, scalar1=lift, scalar2=0.0, op0=ALU.add, op1=ALU.max
+                    )
+                else:
+                    nc.scalar.activation(out=y2[:, :, c, :], in_=by_row, func=ACT.Relu, bias=lift)
+
+        gates = {}
+
+        def gate(unit):
+            slab, first, width = unit
+            s = keep.tile([P, ROWS, width // P, ATOMS], F32, name="gate_%d" % first)
+            for i, c in enumerate(chunks_of(first, width)):
+                nc.scalar.activation(out=s[:, :, i, :], in_=y2[:, :, c, :], func=ACT.Sigmoid, bias=-LIFT2)
+            gates[unit] = s
+
+        def multiply(unit):
             nc.vector.tensor_reduce(
-                out=product[:, :, chunks],
-                in_=gate2[:, chunks, :].rearrange("p c (r j) -> p r c j", j=ATOMS),
+                out=products[:, :, unit_chunks(unit), :].rearrange("p r c q -> p r (c q)"),
+                in_=gates[unit][:].rearrange("p r c (q j) -> p r (c q) j", q=2),
                 axis=AXIS.X,
                 op=ALU.mult,
             )
-        nc.scalar.activation(out=table_warmer[:, 1:2], in_=minus_k[:, 0:1], func=ACT.Ln, scale=0.0, bias=1.0)
+
+        second_matmul(w2_last[0], lift_on_vector=False)
+        second_matmul(w2_last[1], lift_on_vector=False)
+        gate(w2_last[0])
+        gate(w2_last[1])
+        second_matmul(w2_last[3], lift_on_vector=True)
+        second_matmul(w2_last[2], lift_on_vector=True)
+        gate(w2_last[3])
+        gate(w2_last[2])
+        for unit in (w2_last[0], w2_last[1], w2_last[3], w2_last[2]):
+            multiply(unit)
+        product = keep.tile([P, ROWS * CHUNKS], F32)
+        halves = products[:].rearrange("p r c q -> p q (r c)")
+        nc.vector.scalar_tensor_tensor(
+            out=product[:],
+            in0=halves[:, 0, :],
+            scalar=float(2**PRODUCT_SHIFT),
+            in1=halves[:, 1, :],
+            op0=ALU.mult,
+            op1=ALU.mult,
+        )
+        nc.scalar.activation(out=table_warmer[:, 1:2], in_=table_warmer[:, 3:4], func=ACT.Ln, bias=1.0)
 
         sum_rows = banks.tile([P, P], F32, tag="bank")
-        by_atom = positive2[:].rearrange("p r c j -> p j (r c)")
+        by_atom = y2[:].rearrange("p r c j -> p j (r c)")
         product_rows = banks.tile([P, P], F32, tag="bank")
         for j in range(ATOMS):
             nc.tensor.matmul(
@@ -302,16 +324,17 @@ def tile_cfconv_pa_s_kernel(tc, x, distances, W1, b1, W2, b2, out):
                 stop=(j == ATOMS - 1),
                 is_transpose=True,
             )
-        nc.tensor.transpose(out=product_rows[:], in_=product[:].rearrange("p r c -> p (r c)"), identity=ident_f32[:])
+        nc.tensor.transpose(out=product_rows[:], in_=product[:], identity=ident_f32[:])
         log_rows = keep.tile([P, P], F32)
         filter_rows = keep.tile([P, P], F32)
         result = keep.tile([P, P], F32)
         ends = [slice(0, P // 2), slice(P // 2, P)]
+        constant = (PRODUCT_SHIFT - ATOMS) * math.log(2.0) - ATOMS * LIFT2
         for end in ends:
-            nc.scalar.activation(out=log_rows[:, end], in_=product_rows[:, end], func=ACT.Ln, scale=float(2**ATOMS))
+            nc.scalar.activation(out=log_rows[:, end], in_=product_rows[:, end], func=ACT.Ln)
         for end in ends:
             nc.vector.scalar_tensor_tensor(
-                out=filter_rows[:, end], in0=sum_rows[:, end], scalar=0.5, in1=log_rows[:, end], op0=ALU.mult, op1=ALU.subtract
+                out=filter_rows[:, end], in0=sum_rows[:, end], scalar=constant, in1=log_rows[:, end], op0=ALU.add, op1=ALU.subtract
             )
         for end in ends:
             nc.vector.tensor_tensor(out=result[:, end], in0=filter_rows[:, end], in1=x_rows[:, end], op=ALU.mult)

@@ -168,13 +168,14 @@ def tile_cfconv_pa_s_kernel(tc, x, distances, W1, b1, W2, b2, out):
         nc.vector.quantize_mx(
             out=e_codes[:].bitcast(FP8X4), scales=e_scales[:], in_=e_grouped[:].rearrange("p r t -> p (r t)")
         )
-        quantise(*w1_units[1])
         regroup(*w1_units[2])
+        quantise(*w1_units[1])
         first_matmul(w1_units[0])
         first_matmul(w1_units[1])
         quantise(*w1_units[2])
         quantise(*w1_units[3])
         first_matmul(w1_units[2])
+        first_matmul(w1_units[3])
 
         def grow(g):
             chunks = pass_chunks(g)
@@ -183,7 +184,6 @@ def tile_cfconv_pa_s_kernel(tc, x, distances, W1, b1, W2, b2, out):
         w2_first = [(1, 0, BIG), (1, BIG, BIG)]
         w2_last = [(2, first, SMALL) for first in range(0, FEATURES, SMALL)]
         grow(0)
-        first_matmul(w1_units[3])
         grow(1)
         for g in range(PASSES):
             nc.scalar.activation(

@@ -211,10 +211,10 @@ def tile_cfconv_pa_s_kernel(tc, x, distances, W1, b1, W2, b2, out):
         regroup(*w2_first[0])
         regroup(*w2_first[1])
         quantise(*w2_first[0])
-        regroup(*w2_last[0])
+        keep_clock_up(w2_first[0], 2)
+        regroup(2, 0, BIG)
         quantise(*w2_first[1])
         keep_clock_up(w2_first[1], 3)
-        regroup(*w2_last[1])
         quantise(*w2_last[0])
         h_grouped = keep.tile([P, PASSES, PAIRS, PACK], BF16, align_bytes=64)
         h_codes = keep.tile([P, PASSES, PAIRS], U32, align_bytes=64)
@@ -298,18 +298,33 @@ def tile_cfconv_pa_s_kernel(tc, x, distances, W1, b1, W2, b2, out):
         second_matmul(w2_last[2], lift_on_vector=True)
         gate(w2_last[3])
         gate(w2_last[2])
-        for unit in (w2_last[0], w2_last[1], w2_last[3], w2_last[2]):
-            multiply(unit)
-        product = keep.tile([P, ROWS * CHUNKS], F32)
-        halves = products[:].rearrange("p r c q -> p q (r c)")
-        nc.vector.scalar_tensor_tensor(
-            out=product[:],
-            in0=halves[:, 0, :],
-            scalar=float(2**PRODUCT_SHIFT),
-            in1=halves[:, 1, :],
-            op0=ALU.mult,
-            op1=ALU.mult,
+        pairs_of_two = keep.tile([P, ROWS * PACK, 2], F32)
+        first_products = keep.tile([P, ROWS, 2, 2], F32)
+        by_two = gates[w2_last[0]][:].rearrange("p r c (q a b) -> p a (r c q) b", a=2, b=2)
+        nc.gpsimd.tensor_tensor(out=pairs_of_two[:], in0=by_two[:, 0], in1=by_two[:, 1], op=ALU.mult)
+        nc.gpsimd.tensor_tensor(
+            out=first_products[:].rearrange("p r c q -> p (r c q)"),
+            in0=pairs_of_two[:, :, 0],
+            in1=pairs_of_two[:, :, 1],
+            op=ALU.mult,
         )
+        for unit in (w2_last[1], w2_last[3], w2_last[2]):
+            multiply(unit)
+        product = keep.tile([P, ROWS, CHUNKS], F32)
+
+        def join(chunks, halves):
+            nc.vector.scalar_tensor_tensor(
+                out=product[:, :, chunks],
+                in0=halves[:, :, :, 0],
+                scalar=float(2**PRODUCT_SHIFT),
+                in1=halves[:, :, :, 1],
+                op0=ALU.mult,
+                op1=ALU.mult,
+            )
+
+        first_chunks = unit_chunks(w2_last[0])
+        join(first_chunks, first_products)
+        join(slice(first_chunks.stop, CHUNKS), products[:, :, first_chunks.stop :, :])
         nc.scalar.activation(out=table_warmer[:, 1:2], in_=table_warmer[:, 3:4], func=ACT.Ln, bias=1.0)
 
         sum_rows = banks.tile([P, P], F32, tag="bank")
@@ -324,7 +339,10 @@ def tile_cfconv_pa_s_kernel(tc, x, distances, W1, b1, W2, b2, out):
                 stop=(j == ATOMS - 1),
                 is_transpose=True,
             )
-        nc.tensor.transpose(out=product_rows[:], in_=product[:], identity=ident_f32[:])
+            if j == ATOMS - 3:
+                nc.tensor.transpose(
+                    out=product_rows[:], in_=product[:].rearrange("p r c -> p (r c)"), identity=ident_f32[:]
+                )
         log_rows = keep.tile([P, P], F32)
         filter_rows = keep.tile([P, P], F32)
         result = keep.tile([P, P], F32)

@@ -189,6 +189,7 @@ def tile_cfconv_pa_s_kernel(tc, x, distances, W1, b1, W2, b2, out):
             nc.scalar.activation(
                 out=log1[:, pass_chunks(g), :], in_=grown1[:, pass_chunks(g), :], func=ACT.Ln, scale=0.5, bias=0.5
             )
+        slab, first, width = w2_last[2]
         regroup_on_scalar(*w2_last[3])
         nc.scalar.activation(out=table_warmer[:, 0:1], in_=table_warmer[:, 3:4], func=ACT.Sigmoid)
 
@@ -215,7 +216,6 @@ def tile_cfconv_pa_s_kernel(tc, x, distances, W1, b1, W2, b2, out):
         regroup(2, 0, BIG)
         quantise(*w2_first[1])
         keep_clock_up(w2_first[1], 3)
-        quantise(*w2_last[0])
         h_grouped = keep.tile([P, PASSES, PAIRS, PACK], BF16, align_bytes=64)
         h_codes = keep.tile([P, PASSES, PAIRS], U32, align_bytes=64)
         h_scales = keep.tile([P, PASSES, PAIRS], U8, align_bytes=64)
@@ -230,21 +230,18 @@ def tile_cfconv_pa_s_kernel(tc, x, distances, W1, b1, W2, b2, out):
                 op1=ALU.add,
             )
 
-        def h_quantise(g):
-            nc.vector.quantize_mx(
-                out=h_codes[:, g, :].bitcast(FP8X4),
-                scales=h_scales[:, g, :],
-                in_=h_grouped[:, g, :, :].rearrange("p r t -> p (r t)"),
-            )
-
         h_add(0)
         h_add(1)
-        h_quantise(0)
-        h_quantise(1)
+        quantise(2, 0, BIG)
+        nc.vector.quantize_mx(
+            out=h_codes[:].rearrange("p g r -> p (g r)").bitcast(FP8X4),
+            scales=h_scales[:].rearrange("p g r -> p (g r)"),
+            in_=h_grouped[:].rearrange("p g r t -> p (g r t)"),
+        )
         regroup(*w2_last[2])
-        quantise(*w2_last[1])
         quantise(*w2_last[3])
-        quantise(*w2_last[2])
+        for c in chunks_of(first, width):
+            quantise(slab, c * P, P)
 
         y2 = keep.tile([P, ROWS, CHUNKS, ATOMS], F32)
         products = keep.tile([P, ROWS, CHUNKS, 2], F32)

import math

import concourse.mybir as mybir
from concourse.masks import make_identity

F32 = mybir.dt.float32
BF16 = mybir.dt.bfloat16
I32 = mybir.dt.int32
U32 = mybir.dt.uint32
U8 = mybir.dt.uint8
FP8X4 = mybir.dt.float8_e4m3fn_x4
ACT = mybir.ActivationFunctionType
ALU = mybir.AluOpType
AXIS = mybir.AxisListType

P = 128
PACK = 4
K_PASS = P * PACK

ATOMS = 8
ROWS = 16
PAIRS = ROWS * ATOMS
BASIS = 512
FEATURES = 1024
PASSES = FEATURES // K_PASS
CHUNKS = FEATURES // P
SLABS = 1 + PASSES
BIG = 512
SMALL = 256
LIFT1 = 24.0
LIFT2 = 16.0
PRODUCT_SHIFT = 64
RUN = 4

FLOPS = 2 * PAIRS * BASIS * FEATURES + 2 * PAIRS * FEATURES * FEATURES


def chunks_of(first_column, width):
    return range(first_column // P, (first_column + width) // P)


def tile_cfconv_pa_s_kernel(tc, x, distances, W1, b1, W2, b2, out):
    nc = tc.nc
    with tc.tile_pool(name="keep", bufs=1) as keep, tc.psum_pool(name="banks", bufs=8) as banks, tc.manual_schedule():
        table_warmer = keep.tile([P, 4], F32)
        nc.vector.memset(table_warmer[:, 3:4], 0.0)
        nc.scalar.activation(out=table_warmer[:, 2:3], in_=table_warmer[:, 3:4], func=ACT.Exp)

        d_column = keep.tile([P, 1], BF16)
        nc.sync.dma_start(out=d_column[:], in_=distances.rearrange("b i (j o) -> (b i j) o", o=1))

        slab_rows = [
            W1.rearrange("(p t) f -> p t f", t=PACK),
            W2[0:K_PASS, :].rearrange("(t p) f -> p t f", p=P),
            W2[K_PASS : 2 * K_PASS, :].rearrange("(t p) f -> p t f", p=P),
        ]
        raw_tiles = {}

        def load(slab, first, width):
            raw = keep.tile([P, PACK, width], BF16, name="raw_%d_%d" % (slab, first))
            nc.sync.dma_start(out=raw[:], in_=slab_rows[slab][:, :, first : first + width])
            raw_tiles[slab, first, width] = raw

        def raw_columns(slab, first, width):
            for (s, start, loaded), raw in raw_tiles.items():
                if s == slab and start <= first and first + width <= start + loaded:
                    return raw[:, :, first - start : first - start + width]

        w1_units = [(0, first, SMALL) for first in range(0, FEATURES, SMALL)]
        load(*w1_units[0])
        load(*w1_units[1])
        bias_rows = keep.tile([P, P], BF16)
        nc.vector.memset(bias_rows[:], 0.0)
        nc.sync.dma_start(out=bias_rows[0:CHUNKS, :], in_=b1.rearrange("(m p) -> m p", p=P))
        nc.sync.dma_start(out=bias_rows[CHUNKS : 2 * CHUNKS, :], in_=b2.rearrange("(m p) -> m p", p=P))
        load(0, BIG, BIG)
        load(1, 0, BIG)
        load(1, BIG, BIG)
        load(2, 0, BIG)
        load(2, BIG, BIG)
        x_rows = keep.tile([P, P], BF16)
        nc.sync.dma_start(out=x_rows[:], in_=x.rearrange("b i (c p) -> (b i c) p", p=P))

        minus_k_int = keep.tile([P, PACK], I32)
        nc.gpsimd.iota(minus_k_int[:], pattern=[[-1, PACK]], base=0, channel_multiplier=-PACK)
        minus_k = keep.tile([P, PACK], F32)
        nc.vector.tensor_copy(out=minus_k[:], in_=minus_k_int[:])
        ident_bf = keep.tile([P, P], BF16)
        make_identity(nc, ident_bf[:])
        ident_f32 = keep.tile([P, P], F32)
        make_identity(nc, ident_f32[:])

        d_all = banks.tile([P, PAIRS], F32, tag="bank")
        nc.tensor.matmul(out=d_all[:], lhsT=d_column[:, 0:1].to_broadcast([P, P]), rhs=ident_bf[:], start=True, stop=True)
        square = keep.tile([P, PACK, PAIRS], F32)
        for t in range(PACK):
            nc.scalar.activation(
                out=square[:, t, :], in_=d_all[:], func=ACT.Square, scale=10.0, bias=minus_k[:, t : t + 1]
            )
        e_grouped = keep.tile([P, PAIRS, PACK], BF16, align_bytes=64)
        nc.scalar.activation(out=e_grouped[:], in_=square[:].rearrange("p t r -> p r t"), func=ACT.Exp, scale=-0.1)
        e_codes = keep.tile([P, PAIRS], U32, align_bytes=64)
        e_scales = keep.tile([P, PAIRS], U8, align_bytes=64)

        bias_turned = banks.tile([P, P], BF16, tag="bank")
        nc.tensor.transpose(out=bias_turned[:], in_=bias_rows[:], identity=ident_bf[:])
        lifted = keep.tile([P, 2 * CHUNKS], F32)
        layer1, layer2 = slice(0, CHUNKS), slice(CHUNKS, 2 * CHUNKS)
        nc.scalar.activation(out=lifted[:, layer1], in_=bias_turned[:, layer1], func=ACT.Identity, bias=LIFT1)
        nc.scalar.activation(out=lifted[:, layer2], in_=bias_turned[:, layer2], func=ACT.Identity, bias=LIFT2)

        grouped = keep.tile([P, SLABS, FEATURES, PACK], BF16, align_bytes=64)
        w_codes = keep.tile([P, SLABS, FEATURES], U32, align_bytes=64)
        w_scales = keep.tile([P, SLABS, FEATURES], U8, align_bytes=64)

        def regroup(slab, first, width):
            cols = slice(first, first + width)
            nc.vector.tensor_copy(
                out=grouped[:, slab, cols, :].rearrange("p (c i) t -> p c t i", i=RUN),
                in_=raw_columns(slab, first, width).rearrange("p t (c i) -> p c t i", i=RUN),
            )

        def regroup_on_scalar(slab, first, width):
            cols = slice(first, first + width)
            nc.scalar.copy(
                out=grouped[:, slab, cols, :].rearrange("p (c i) t -> p c t i", i=RUN),
                in_=raw_columns(slab, first, width).rearrange("p t (c i) -> p c t i", i=RUN),
            )

        def quantise(slab, first, width):
            cols = slice(first, first + width)
            nc.vector.quantize_mx(
                out=w_codes[:, slab, cols].bitcast(FP8X4),
                scales=w_scales[:, slab, cols],
                in_=grouped[:, slab, cols, :].rearrange("p c t -> p (c t)"),
            )

        y1 = keep.tile([P, CHUNKS, PAIRS], F32)
        grown1 = keep.tile([P, CHUNKS, PAIRS], F32)
        log1 = keep.tile([P, CHUNKS, PAIRS], F32)

        def first_matmul(unit):
            slab, first, width = unit
            for m in chunks_of(first, width):
                m_cols = slice(m * P, (m + 1) * P)
                v1 = banks.tile([P, PAIRS], F32, tag="bank")
                nc.tensor.matmul_mx(
                    out=v1[:],
                    lhsT=w_codes[:, slab, m_cols].bitcast(FP8X4),
                    lhsT_scale=w_scales[:, slab, m_cols],
                    rhs=e_codes[:].bitcast(FP8X4),
                    rhs_scale=e_scales[:],
                    start=True,
                    stop=True,
                )
                nc.scalar.activation(out=y1[:, m, :], in_=v1[:], func=ACT.Relu, bias=lifted[:, m : m + 1])

        def pass_chunks(g):
            return slice(g * PACK, (g + 1) * PACK)

        def unit_chunks(unit):
            return slice(unit[1] // P, (unit[1] + unit[2]) // P)

        regroup_on_scalar(*w1_units[3])
        regroup(*w1_units[0])
        regroup(*w1_units[1])
        quantise(*w1_units[0])
        nc.vector.quantize_mx(
            out=e_codes[:].bitcast(FP8X4), scales=e_scales[:], in_=e_grouped[:].rearrange("p r t -> p (r t)")
        )
        regroup(*w1_units[2])
        quantise(*w1_units[1])
        first_matmul(w1_units[0])
        first_matmul(w1_units[1])
        quantise(*w1_units[2])
        quantise(*w1_units[3])
        first_matmul(w1_units[2])
        first_matmul(w1_units[3])

        def grow(g):
            chunks = pass_chunks(g)
            nc.scalar.activation(out=grown1[:, chunks, :], in_=y1[:, chunks, :], func=ACT.Exp, scale=-1.0, bias=LIFT1)

        w2_first = [(1, 0, BIG), (1, BIG, BIG)]
        w2_last = [(2, first, SMALL) for first in range(0, FEATURES, SMALL)]
        grow(0)
        grow(1)
        for g in range(PASSES):
            nc.scalar.activation(
                out=log1[:, pass_chunks(g), :], in_=grown1[:, pass_chunks(g), :], func=ACT.Ln, scale=0.5, bias=0.5
            )
        slab, first, width = w2_last[2]
        regroup_on_scalar(*w2_last[3])
        nc.scalar.activation(out=table_warmer[:, 0:1], in_=table_warmer[:, 3:4], func=ACT.Sigmoid)

        spin = banks.tile([P, BIG], F32, tag="bank")

        def keep_clock_up(unit, count):
            slab, first, width = unit
            cols = slice(first, first + width)
            for i in range(count):
                nc.tensor.matmul_mx(
                    out=spin[:],
                    lhsT=w_codes[:, 0, 0:P].bitcast(FP8X4),
                    lhsT_scale=w_scales[:, 0, 0:P],
                    rhs=w_codes[:, slab, cols].bitcast(FP8X4),
                    rhs_scale=w_scales[:, slab, cols],
                    start=True,
                    stop=True,
                )

        regroup(*w2_first[0])
        regroup(*w2_first[1])
        quantise(*w2_first[0])
        keep_clock_up(w2_first[0], 2)
        regroup(2, 0, BIG)
        quantise(*w2_first[1])
        keep_clock_up(w2_first[1], 3)
        h_grouped = keep.tile([P, PASSES, PAIRS, PACK], BF16, align_bytes=64)
        h_codes = keep.tile([P, PASSES, PAIRS], U32, align_bytes=64)
        h_scales = keep.tile([P, PASSES, PAIRS], U8, align_bytes=64)

        def h_add(g):
            nc.vector.scalar_tensor_tensor(
                out=h_grouped[:, g, :, :],
                in0=y1[:, pass_chunks(g), :].rearrange("p t r -> p r t"),
                scalar=-LIFT1,
                in1=log1[:, pass_chunks(g), :].rearrange("p t r -> p r t"),
                op0=ALU.add,
                op1=ALU.add,
            )

        h_add(0)
        h_add(1)
        quantise(2, 0, BIG)
        nc.vector.quantize_mx(
            out=h_codes[:].rearrange("p g r -> p (g r)").bitcast(FP8X4),
            scales=h_scales[:].rearrange("p g r -> p (g r)"),
            in_=h_grouped[:].rearrange("p g r t -> p (g r t)"),
        )
        regroup(*w2_last[2])
        quantise(*w2_last[3])
        for c in chunks_of(first, width):
            quantise(slab, c * P, P)

        y2 = keep.tile([P, ROWS, CHUNKS, ATOMS], F32)
        products = keep.tile([P, ROWS, CHUNKS, 2], F32)

        def second_matmul(unit, lift_on_vector):
            slab, first, width = unit
            for c in chunks_of(first, width):
                c_cols = slice(c * P, (c + 1) * P)
                v2 = banks.tile([P, PAIRS], F32, tag="bank")
                for g in range(PASSES):
                    nc.tensor.matmul_mx(
                        out=v2[:],
                        lhsT=w_codes[:, 1 + g, c_cols].bitcast(FP8X4),
                        lhsT_scale=w_scales[:, 1 + g, c_cols],
                        rhs=h_codes[:, g, :].bitcast(FP8X4),
                        rhs_scale=h_scales[:, g, :],
                        start=(g == 0),
                        stop=(g == PASSES - 1),
                    )
                by_row = v2[:].rearrange("p (r j) -> p r j", j=ATOMS)
                lift = lifted[:, CHUNKS + c : CHUNKS + c + 1]
                if lift_on_vector:
                    nc.vector.tensor_scalar(
                        out=y2[:, :, c, :], in0=by_row, scalar1=lift, scalar2=0.0, op0=ALU.add, op1=ALU.max
                    )
                else:
                    nc.scalar.activation(out=y2[:, :, c, :], in_=by_row, func=ACT.Relu, bias=lift)

        gates = {}

        def gate(unit):
            slab, first, width = unit
            s = keep.tile([P, ROWS, width // P, ATOMS], F32, name="gate_%d" % first)
            for i, c in enumerate(chunks_of(first, width)):
                nc.scalar.activation(out=s[:, :, i, :], in_=y2[:, :, c, :], func=ACT.Sigmoid, bias=-LIFT2)
            gates[unit] = s

        def multiply(unit):
            nc.vector.tensor_reduce(
                out=products[:, :, unit_chunks(unit), :].rearrange("p r c q -> p r (c q)"),
                in_=gates[unit][:].rearrange("p r c (q j) -> p r (c q) j", q=2),
                axis=AXIS.X,
                op=ALU.mult,
            )

        second_matmul(w2_last[0], lift_on_vector=False)
        second_matmul(w2_last[1], lift_on_vector=False)
        gate(w2_last[0])
        gate(w2_last[1])
        second_matmul(w2_last[3], lift_on_vector=True)
        second_matmul(w2_last[2], lift_on_vector=True)
        gate(w2_last[3])
        gate(w2_last[2])
        pairs_of_two = keep.tile([P, ROWS * PACK, 2], F32)
        first_products = keep.tile([P, ROWS, 2, 2], F32)
        by_two = gates[w2_last[0]][:].rearrange("p r c (q a b) -> p a (r c q) b", a=2, b=2)
        nc.gpsimd.tensor_tensor(out=pairs_of_two[:], in0=by_two[:, 0], in1=by_two[:, 1], op=ALU.mult)
        nc.gpsimd.tensor_tensor(
            out=first_products[:].rearrange("p r c q -> p (r c q)"),
            in0=pairs_of_two[:, :, 0],
            in1=pairs_of_two[:, :, 1],
            op=ALU.mult,
        )
        for unit in (w2_last[1], w2_last[3], w2_last[2]):
            multiply(unit)
        product = keep.tile([P, ROWS, CHUNKS], F32)

        def join(chunks, halves):
            nc.vector.scalar_tensor_tensor(
                out=product[:, :, chunks],
                in0=halves[:, :, :, 0],
                scalar=float(2**PRODUCT_SHIFT),
                in1=halves[:, :, :, 1],
                op0=ALU.mult,
                op1=ALU.mult,
            )

        first_chunks = unit_chunks(w2_last[0])
        join(first_chunks, first_products)
        join(slice(first_chunks.stop, CHUNKS), products[:, :, first_chunks.stop :, :])
        nc.scalar.activation(out=table_warmer[:, 1:2], in_=table_warmer[:, 3:4], func=ACT.Ln, bias=1.0)

        sum_rows = banks.tile([P, P], F32, tag="bank")
        by_atom = y2[:].rearrange("p r c j -> p j (r c)")
        product_rows = banks.tile([P, P], F32, tag="bank")
        for j in range(ATOMS):
            nc.tensor.matmul(
                out=sum_rows[:],
                lhsT=by_atom[:, j, :],
                rhs=ident_f32[:],
                start=(j == 0),
                stop=(j == ATOMS - 1),
                is_transpose=True,
            )
            if j == ATOMS - 3:
                nc.tensor.transpose(
                    out=product_rows[:], in_=product[:].rearrange("p r c -> p (r c)"), identity=ident_f32[:]
                )
        log_rows = keep.tile([P, P], F32)
        filter_rows = keep.tile([P, P], F32)
        result = keep.tile([P, P], F32)
        ends = [slice(0, P // 2), slice(P // 2, P)]
        constant = (PRODUCT_SHIFT - ATOMS) * math.log(2.0) - ATOMS * LIFT2
        for end in ends:
            nc.scalar.activation(out=log_rows[:, end], in_=product_rows[:, end], func=ACT.Ln)
        for end in ends:
            nc.vector.scalar_tensor_tensor(
                out=filter_rows[:, end], in0=sum_rows[:, end], scalar=constant, in1=log_rows[:, end], op0=ALU.add, op1=ALU.subtract
            )
        for end in ends:
            nc.vector.tensor_tensor(out=result[:, end], in0=filter_rows[:, end], in1=x_rows[:, end], op=ALU.mult)
        out_rows = out.rearrange("b i (c p) -> (b i c) p", p=P)
        nc.sync.dma_start(out=out_rows[:, ends[0]], in_=result[:, ends[0]])
        nc.scalar.dma_start(out=out_rows[:, ends[1]], in_=result[:, ends[1]])
